import numpy as np
import ml_dtypes


def mxq(x, axis, fmt="e4m3"):
    dtype, down = {"e4m3": (ml_dtypes.float8_e4m3fn, 7), "e5m2": (ml_dtypes.float8_e5m2, 14)}[fmt]
    v = np.moveaxis(np.asarray(x, np.float32).astype(ml_dtypes.bfloat16).astype(np.float64), axis, -1)
    blocks = v.reshape(v.shape[:-1] + (-1, 32))
    amax = np.abs(blocks).max(-1, keepdims=True)
    byte = np.maximum(np.where(amax > 0, np.frexp(amax)[1] - 1 + 127, 0) - down, 1)
    scale = np.exp2(byte - 127.0)
    codes = (blocks / scale).astype(np.float32).astype(dtype).astype(np.float64)
    return np.moveaxis((codes * scale).reshape(v.shape), -1, axis)


WIDE = False


def mx_kscale(k):
    if not WIDE:
        return np.ones(k)
    levels = np.array([10, -10, 5, -5, 0])
    a = np.random.permutation(np.resize(levels, k // 512 * 4)).reshape(k // 512, 4)
    idx = np.arange(k)
    return np.exp2(a[idx // 512, idx % 128 // 32])


BF16 = ml_dtypes.bfloat16


def bf(x):
    return np.asarray(x, np.float32).astype(BF16)


def f64(x):
    return np.asarray(x).astype(np.float64)


B, N, IN_DIM, UNITS, K = 8, 1024, 128, 128, 3
F = IN_DIM + UNITS
NUM_MX = K + 1
ROWS = F * NUM_MX


def sigmoid(v):
    return 1.0 / (1.0 + np.exp(-v))


def setup_inputs():
    tf = mx_kscale(ROWS)[::NUM_MX]
    tr = np.repeat(tf, NUM_MX)[:, None]
    return {"adj": bf(np.random.standard_normal((N, N)) * 0.5 / np.sqrt(N)),
            "x0": bf(np.random.standard_normal((B, N, F)) * tf),
            "x1": bf(np.random.standard_normal((B, N, F)) * 0.5 * tf),
            "x2": bf(np.random.standard_normal((B, N, F)) * 1.1 * tf),
            "h_prev": bf(np.random.standard_normal((B, N * UNITS))),
            "r_kernel": bf(np.random.standard_normal((ROWS, UNITS)) / np.sqrt(ROWS) / tr),
            "r_bias": bf(np.random.standard_normal(UNITS) * 0.3),
            "u_kernel": bf(np.random.standard_normal((ROWS, UNITS)) / np.sqrt(ROWS) / tr),
            "u_bias": bf(np.random.standard_normal(UNITS) * 0.3)}


def reference(adj, x0, x1, x2, h_prev, r_kernel, r_bias, u_kernel, u_bias):
    x0, x1, x2 = f64(x0), f64(x1), f64(x2)
    x3 = 2.0 * (mxq(f64(adj), 1, "e4m3") @ mxq(x2, 1, "e4m3")) - x1
    xk = np.stack([x0, x1, x2, x3], axis=-1).reshape(B * N, ROWS)
    xq = mxq(xk, 1, "e4m3")
    r = sigmoid((xq @ mxq(f64(r_kernel), 0, "e4m3")) + f64(r_bias))
    u = sigmoid((xq @ mxq(f64(u_kernel), 0, "e4m3")) + f64(u_bias))
    rh = r.reshape(B, N, UNITS) * f64(h_prev).reshape(B, N, UNITS)
    return rh, u.reshape(B, N * UNITS)

@@ -1,0 +1,228 @@
+from contextlib import ExitStack
+
+import concourse.mybir as mybir
+from concourse.masks import make_identity
+
+BF16 = mybir.dt.bfloat16
+F32 = mybir.dt.float32
+U32 = mybir.dt.uint32
+U8 = mybir.dt.uint8
+FP8X4 = mybir.dt.float8_e4m3fn_x4
+ALU = mybir.AluOpType
+ACT = mybir.ActivationFunctionType
+
+P = 128
+PACK = 4
+BATCH = 8
+NODES = 1024
+FEATS = 256
+UNITS = 128
+TERMS = 4
+PASSES = 2
+SLOTS = NODES // P
+GATES = 2
+
+FLOPS = 2 * BATCH * NODES * NODES * FEATS + 2 * BATCH * NODES * (TERMS * FEATS) * (GATES * UNITS)
+
+
+def by_node(rows):
+    return rows.rearrange("(g p t) w -> p g (t w)", g=PASSES, p=P, t=PACK)
+
+
+def tile_gts_gcgrucell_pb_t_kernel(
+    tc, adj, x0, x1, x2, h_prev, r_kernel, r_bias, u_kernel, u_bias, out_0, out_1
+):
+    nc = tc.nc
+    with ExitStack() as ctx:
+        const = ctx.enter_context(tc.tile_pool(name="const", bufs=1))
+        loads = ctx.enter_context(tc.tile_pool(name="loads", bufs=4))
+        work = ctx.enter_context(tc.tile_pool(name="work", bufs=2))
+        outs = ctx.enter_context(tc.tile_pool(name="outs", bufs=3))
+        ps_flip = ctx.enter_context(tc.psum_pool(name="ps_flip", bufs=4))
+        ps_diff = ctx.enter_context(tc.psum_pool(name="ps_diff", bufs=2))
+        ps_gate = ctx.enter_context(tc.psum_pool(name="ps_gate", bufs=2))
+
+        x_dram = [x0, x1, x2]
+        h_rows = h_prev.rearrange("b (n j) -> b n j", j=UNITS)
+        u_rows = out_1.rearrange("b (n j) -> b n j", j=UNITS)
+
+        def load_terms(b):
+            terms = {}
+            for k in (2, 1, 0):
+                x_sb = loads.tile([P, SLOTS, FEATS], BF16, name="x%d_sb" % k)
+                nc.sync.dma_start(
+                    out=x_sb[:].rearrange("p (g t) f -> p g (t f)", g=PASSES), in_=by_node(x_dram[k][b])
+                )
+                terms[k] = x_sb
+            return terms
+
+        def load_state(b):
+            h_sb = loads.tile([P, SLOTS, UNITS], BF16)
+            nc.sync.dma_start(
+                out=h_sb[:].rearrange("p (g t) j -> p g (t j)", g=PASSES), in_=by_node(h_rows[b])
+            )
+            return h_sb
+
+        adj_sb = const.tile([P, PASSES, PACK * NODES], BF16)
+        for g in range(PASSES):
+            nc.sync.dma_start(out=adj_sb[:, g, :], in_=by_node(adj)[:, g, :])
+        terms_of = {0: load_terms(0)}
+        w_raw = const.tile([P, GATES, PASSES, PACK, UNITS], BF16)
+        for gate, kernel in enumerate((r_kernel, u_kernel)):
+            nc.sync.dma_start(
+                out=w_raw[:, gate].rearrange("p c t j -> p c (t j)"),
+                in_=kernel.rearrange("(c p t) j -> p c (t j)", c=PASSES, p=P, t=PACK),
+            )
+        bias_bc = const.tile([P, GATES * UNITS], BF16)
+        nc.sync.dma_start(out=bias_bc[:, 0:UNITS], in_=r_bias.partition_broadcast(P))
+        nc.sync.dma_start(out=bias_bc[:, UNITS : 2 * UNITS], in_=u_bias.partition_broadcast(P))
+        terms_of[1] = load_terms(1)
+
+        ident_bf = const.tile([P, P], BF16)
+        make_identity(nc, ident_bf[:])
+        ident_f32 = const.tile([P, P], F32)
+        make_identity(nc, ident_f32[:])
+
+        adj_words = adj_sb[:].rearrange("p g w -> p (g w)").bitcast(F32).rearrange(
+            "p (s c q u) -> p s c u q", s=SLOTS, c=PASSES, q=P, u=2
+        )
+        adj_grouped = const.tile([P, SLOTS * PASSES * P * PACK], BF16, align_bytes=64)
+        adj_grouped_words = adj_grouped[:].bitcast(F32).rearrange(
+            "q (s c n u) -> q s c n u", s=SLOTS, c=PASSES, n=P, u=2
+        )
+        adj_codes = const.tile([P, SLOTS, PASSES, P], U32, align_bytes=64)
+        adj_scales = const.tile([P, SLOTS, PASSES, P], U8, align_bytes=64)
+        slot_cols = PASSES * P * PACK
+        for s in range(SLOTS):
+            flipped = ps_flip.tile([P, PASSES, 2, P], F32, tag="flip")
+            for c in range(PASSES):
+                for u in range(2):
+                    nc.tensor.transpose(flipped[:, c, u, :], adj_words[:, s, c, u, :], ident_f32[:])
+            copy = nc.vector.tensor_copy if s % 2 == 0 else nc.scalar.copy
+            copy(out=adj_grouped_words[:, s], in_=flipped[:].rearrange("q c u n -> q c n u"))
+            if s % 2 == 1:
+                nc.vector.quantize_mx(
+                    out=adj_codes[:, s - 1 : s + 1].rearrange("q s c n -> q (s c n)").bitcast(FP8X4),
+                    scales=adj_scales[:, s - 1 : s + 1].rearrange("q s c n -> q (s c n)"),
+                    in_=adj_grouped[:, (s - 1) * slot_cols : (s + 1) * slot_cols],
+                )
+
+        w_grouped = const.tile([P, PASSES, GATES, UNITS, PACK], BF16, align_bytes=64)
+        for c in range(PASSES):
+            for gate in range(GATES):
+                nc.vector.tensor_copy(
+                    out=w_grouped[:, c, gate], in_=w_raw[:, gate, c].rearrange("p t j -> p j t")
+                )
+        w_codes = const.tile([P, PASSES, GATES * UNITS], U32, align_bytes=64)
+        w_scales = const.tile([P, PASSES, GATES * UNITS], U8, align_bytes=64)
+        nc.vector.quantize_mx(
+            out=w_codes[:].rearrange("p c j -> p (c j)").bitcast(FP8X4),
+            scales=w_scales[:].rearrange("p c j -> p (c j)"),
+            in_=w_grouped[:].rearrange("p c g j t -> p (c g j t)"),
+        )
+
+        def diffuse(b):
+            x1_sb, x2_sb = terms_of[b][1], terms_of[b][2]
+            x2_grouped = work.tile([P, PASSES, FEATS, PACK], BF16, align_bytes=64)
+            nc.vector.tensor_copy(
+                out=x2_grouped[:],
+                in_=x2_sb[:].rearrange("p (g t) f -> p g f t", g=PASSES),
+            )
+            x2_codes = work.tile([P, PASSES, FEATS], U32, align_bytes=64)
+            x2_scales = work.tile([P, PASSES, FEATS], U8, align_bytes=64)
+            nc.vector.quantize_mx(
+                out=x2_codes[:].rearrange("p g f -> p (g f)").bitcast(FP8X4),
+                scales=x2_scales[:].rearrange("p g f -> p (g f)"),
+                in_=x2_grouped[:].rearrange("p g f t -> p (g f t)"),
+            )
+            x3_sb = work.tile([P, SLOTS, FEATS], BF16)
+            for s0 in range(0, SLOTS, 2):
+                spread = ps_diff.tile([P, 2, FEATS], F32)
+                for i in range(2):
+                    for c in range(PASSES):
+                        nc.tensor.matmul_mx(
+                            out=spread[:, i, :],
+                            lhsT=adj_codes[:, s0 + i, c, :].bitcast(FP8X4),
+                            lhsT_scale=adj_scales[:, s0 + i, c, :],
+                            rhs=x2_codes[:, c, :].bitcast(FP8X4),
+                            rhs_scale=x2_scales[:, c, :],
+                            start=(c == 0),
+                            stop=(c == PASSES - 1),
+                        )
+                nc.vector.scalar_tensor_tensor(
+                    out=x3_sb[:, s0 : s0 + 2, :],
+                    in0=spread[:],
+                    scalar=2.0,
+                    in1=x1_sb[:, s0 : s0 + 2, :],
+                    op0=ALU.mult,
+                    op1=ALU.subtract,
+                )
+            terms_of[b][3] = x3_sb
+
+        def pack(b):
+            xk_grouped = work.tile([P, SLOTS, PASSES, P, TERMS], BF16, align_bytes=64)
+            xk_codes = work.tile([P, SLOTS, PASSES, P], U32, align_bytes=64)
+            xk_scales = work.tile([P, SLOTS, PASSES, P], U8, align_bytes=64)
+            for s in range(SLOTS):
+                flipped = ps_flip.tile([P, PASSES, TERMS, P], BF16, tag="flip")
+                for c in range(PASSES):
+                    for k in range(TERMS):
+                        nc.tensor.transpose(
+                            flipped[:, c, k, :], terms_of[b][k][:, s, c * P : (c + 1) * P], ident_bf[:]
+                        )
+                copy = nc.vector.tensor_copy if s == SLOTS - 1 else nc.scalar.copy
+                copy(out=xk_grouped[:, s], in_=flipped[:].rearrange("f c k n -> f c n k"))
+                if s % 2 == 1:
+                    nc.vector.quantize_mx(
+                        out=xk_codes[:, s - 1 : s + 1].rearrange("f s c n -> f (s c n)").bitcast(FP8X4),
+                        scales=xk_scales[:, s - 1 : s + 1].rearrange("f s c n -> f (s c n)"),
+                        in_=xk_grouped[:, s - 1 : s + 1].rearrange("f s c n k -> f (s c n k)"),
+                    )
+            return xk_codes, xk_scales
+
+        def gates(b, xk_codes, xk_scales, h_sb):
+            result = outs.tile([P, GATES, SLOTS, UNITS], F32)
+            for s0 in range(0, SLOTS, 2):
+                summed = ps_gate.tile([P, 2, GATES * UNITS], F32)
+                for i in range(2):
+                    for c in range(PASSES):
+                        nc.tensor.matmul_mx(
+                            out=summed[:, i, :],
+                            lhsT=xk_codes[:, s0 + i, c, :].bitcast(FP8X4),
+                            lhsT_scale=xk_scales[:, s0 + i, c, :],
+                            rhs=w_codes[:, c, :].bitcast(FP8X4),
+                            rhs_scale=w_scales[:, c, :],
+                            start=(c == 0),
+                            stop=(c == PASSES - 1),
+                        )
+                biased = outs.tile([P, 2, GATES * UNITS], F32)
+                nc.vector.tensor_tensor(
+                    out=biased[:],
+                    in0=summed[:],
+                    in1=bias_bc[:].unsqueeze(1).to_broadcast([P, 2, GATES * UNITS]),
+                    op=ALU.add,
+                )
+                nc.scalar.activation(
+                    out=result[:, :, s0 : s0 + 2, :].rearrange("p g s j -> p s g j"),
+                    in_=biased[:].rearrange("p s (g j) -> p s g j", g=GATES),
+                    func=ACT.Sigmoid,
+                )
+            nc.gpsimd.tensor_tensor(out=result[:, 0], in0=result[:, 0], in1=h_sb[:], op=ALU.mult)
+            for gate, rows in enumerate((out_0[b], u_rows[b])):
+                nc.sync.dma_start(
+                    out=by_node(rows), in_=result[:, gate].rearrange("p (g t) j -> p g (t j)", g=PASSES)
+                )
+
+        packed_of = {}
+        state_of = {}
+        for step in range(BATCH + 2):
+            if step + 2 < BATCH:
+                terms_of[step + 2] = load_terms(step + 2)
+            if step < BATCH:
+                state_of[step] = load_state(step)
+                diffuse(step)
+            if 1 <= step <= BATCH:
+                packed_of[step - 1] = pack(step - 1)
+            if step >= 2:
+                codes, scales = packed_of[step - 2]
+                gates(step - 2, codes, scales, state_of[step - 2])

@@ -41,32 +41,61 @@ def tile_gts_gcgrucell_pb_t_kernel(
         ps_flip = ctx.enter_context(tc.psum_pool(name="ps_flip", bufs=4))
         ps_diff = ctx.enter_context(tc.psum_pool(name="ps_diff", bufs=2))
         ps_gate = ctx.enter_context(tc.psum_pool(name="ps_gate", bufs=2))
+        ctx.enter_context(tc.manual_schedule())
 
         x_dram = [x0, x1, x2]
         h_rows = h_prev.rearrange("b (n j) -> b n j", j=UNITS)
-        u_rows = out_1.rearrange("b (n j) -> b n j", j=UNITS)
+        out_rows = [out_0, out_1.rearrange("b (n j) -> b n j", j=UNITS)]
 
-        def load_terms(b):
-            terms = {}
+        terms_of = {}
+        state_of = {}
+        x2_mx_of = {}
+        flipped_of = {}
+        xk_of = {}
+        summed_of = {}
+        result_of = {}
+
+        def load_term(b, k):
+            x_sb = loads.tile([P, SLOTS, FEATS], BF16, name="x%d_sb" % k)
+            nc.sync.dma_start(
+                out=x_sb[:].rearrange("p (g t) f -> p g (t f)", g=PASSES), in_=by_node(x_dram[k][b])
+            )
+            terms_of[b][k] = x_sb
+
+        def load_batch(b):
+            terms_of[b] = {}
             for k in (2, 1, 0):
-                x_sb = loads.tile([P, SLOTS, FEATS], BF16, name="x%d_sb" % k)
-                nc.sync.dma_start(
-                    out=x_sb[:].rearrange("p (g t) f -> p g (t f)", g=PASSES), in_=by_node(x_dram[k][b])
-                )
-                terms[k] = x_sb
-            return terms
-
-        def load_state(b):
+                load_term(b, k)
             h_sb = loads.tile([P, SLOTS, UNITS], BF16)
             nc.sync.dma_start(
                 out=h_sb[:].rearrange("p (g t) j -> p g (t j)", g=PASSES), in_=by_node(h_rows[b])
             )
-            return h_sb
+            state_of[b] = h_sb
 
+        def quantise_x2(b):
+            x2_sb = terms_of[b][2]
+            x2_grouped = work.tile([P, PASSES, FEATS, PACK], BF16, align_bytes=64)
+            for g in range(PASSES):
+                nc.vector.tensor_copy(
+                    out=x2_grouped[:, g].rearrange("p (c i) t -> p c t i", i=4),
+                    in_=x2_sb[:, g * PACK : (g + 1) * PACK, :].rearrange("p t (c i) -> p c t i", i=4),
+                )
+            x2_codes = work.tile([P, PASSES, FEATS], U32, align_bytes=64)
+            x2_scales = work.tile([P, PASSES, FEATS], U8, align_bytes=64)
+            nc.vector.quantize_mx(
+                out=x2_codes[:].rearrange("p g f -> p (g f)").bitcast(FP8X4),
+                scales=x2_scales[:].rearrange("p g f -> p (g f)"),
+                in_=x2_grouped[:].rearrange("p g f t -> p (g f t)"),
+            )
+            x2_mx_of[b] = (x2_codes, x2_scales)
+
+        terms_of[0] = {}
+        load_term(0, 2)
         adj_sb = const.tile([P, PASSES, PACK * NODES], BF16)
         for g in range(PASSES):
             nc.sync.dma_start(out=adj_sb[:, g, :], in_=by_node(adj)[:, g, :])
-        terms_of = {0: load_terms(0)}
+        load_term(0, 1)
+        load_term(0, 0)
         w_raw = const.tile([P, GATES, PASSES, PACK, UNITS], BF16)
         for gate, kernel in enumerate((r_kernel, u_kernel)):
             nc.sync.dma_start(
@@ -76,12 +105,19 @@ def tile_gts_gcgrucell_pb_t_kernel(
         bias_bc = const.tile([P, GATES * UNITS], BF16)
         nc.sync.dma_start(out=bias_bc[:, 0:UNITS], in_=r_bias.partition_broadcast(P))
         nc.sync.dma_start(out=bias_bc[:, UNITS : 2 * UNITS], in_=u_bias.partition_broadcast(P))
-        terms_of[1] = load_terms(1)
+        h0_sb = loads.tile([P, SLOTS, UNITS], BF16, name="h_sb")
+        nc.sync.dma_start(
+            out=h0_sb[:].rearrange("p (g t) j -> p g (t j)", g=PASSES), in_=by_node(h_rows[0])
+        )
+        state_of[0] = h0_sb
+        load_batch(1)
 
-        ident_bf = const.tile([P, P], BF16)
-        make_identity(nc, ident_bf[:])
         ident_f32 = const.tile([P, P], F32)
         make_identity(nc, ident_f32[:])
+        ident_bf = const.tile([P, P], BF16)
+        make_identity(nc, ident_bf[:])
+
+        quantise_x2(0)
 
         adj_words = adj_sb[:].rearrange("p g w -> p (g w)").bitcast(F32).rearrange(
             "p (s c q u) -> p s c u q", s=SLOTS, c=PASSES, q=P, u=2
@@ -94,12 +130,12 @@ def tile_gts_gcgrucell_pb_t_kernel(
         adj_scales = const.tile([P, SLOTS, PASSES, P], U8, align_bytes=64)
         slot_cols = PASSES * P * PACK
         for s in range(SLOTS):
-            flipped = ps_flip.tile([P, PASSES, 2, P], F32, tag="flip")
+            adj_flipped = ps_flip.tile([P, PASSES, 2, P], F32, tag="flip")
             for c in range(PASSES):
                 for u in range(2):
-                    nc.tensor.transpose(flipped[:, c, u, :], adj_words[:, s, c, u, :], ident_f32[:])
+                    nc.tensor.transpose(adj_flipped[:, c, u, :], adj_words[:, s, c, u, :], ident_f32[:])
             copy = nc.vector.tensor_copy if s % 2 == 0 else nc.scalar.copy
-            copy(out=adj_grouped_words[:, s], in_=flipped[:].rearrange("q c u n -> q c n u"))
+            copy(out=adj_grouped_words[:, s], in_=adj_flipped[:].rearrange("q c u n -> q c n u"))
             if s % 2 == 1:
                 nc.vector.quantize_mx(
                     out=adj_codes[:, s - 1 : s + 1].rearrange("q s c n -> q (s c n)").bitcast(FP8X4),
@@ -108,121 +144,143 @@ def tile_gts_gcgrucell_pb_t_kernel(
                 )
 
         w_grouped = const.tile([P, PASSES, GATES, UNITS, PACK], BF16, align_bytes=64)
-        for c in range(PASSES):
-            for gate in range(GATES):
-                nc.vector.tensor_copy(
-                    out=w_grouped[:, c, gate], in_=w_raw[:, gate, c].rearrange("p t j -> p j t")
-                )
         w_codes = const.tile([P, PASSES, GATES * UNITS], U32, align_bytes=64)
         w_scales = const.tile([P, PASSES, GATES * UNITS], U8, align_bytes=64)
-        nc.vector.quantize_mx(
-            out=w_codes[:].rearrange("p c j -> p (c j)").bitcast(FP8X4),
-            scales=w_scales[:].rearrange("p c j -> p (c j)"),
-            in_=w_grouped[:].rearrange("p c g j t -> p (c g j t)"),
-        )
 
-        def diffuse(b):
-            x1_sb, x2_sb = terms_of[b][1], terms_of[b][2]
-            x2_grouped = work.tile([P, PASSES, FEATS, PACK], BF16, align_bytes=64)
-            nc.vector.tensor_copy(
-                out=x2_grouped[:],
-                in_=x2_sb[:].rearrange("p (g t) f -> p g f t", g=PASSES),
-            )
-            x2_codes = work.tile([P, PASSES, FEATS], U32, align_bytes=64)
-            x2_scales = work.tile([P, PASSES, FEATS], U8, align_bytes=64)
+        def quantise_kernels():
+            for c in range(PASSES):
+                for gate in range(GATES):
+                    nc.vector.tensor_copy(
+                        out=w_grouped[:, c, gate], in_=w_raw[:, gate, c].rearrange("p t j -> p j t")
+                    )
             nc.vector.quantize_mx(
-                out=x2_codes[:].rearrange("p g f -> p (g f)").bitcast(FP8X4),
-                scales=x2_scales[:].rearrange("p g f -> p (g f)"),
-                in_=x2_grouped[:].rearrange("p g f t -> p (g f t)"),
+                out=w_codes[:].rearrange("p c j -> p (c j)").bitcast(FP8X4),
+                scales=w_scales[:].rearrange("p c j -> p (c j)"),
+                in_=w_grouped[:].rearrange("p c g j t -> p (c g j t)"),
             )
-            x3_sb = work.tile([P, SLOTS, FEATS], BF16)
-            for s0 in range(0, SLOTS, 2):
-                spread = ps_diff.tile([P, 2, FEATS], F32)
-                for i in range(2):
-                    for c in range(PASSES):
-                        nc.tensor.matmul_mx(
-                            out=spread[:, i, :],
-                            lhsT=adj_codes[:, s0 + i, c, :].bitcast(FP8X4),
-                            lhsT_scale=adj_scales[:, s0 + i, c, :],
-                            rhs=x2_codes[:, c, :].bitcast(FP8X4),
-                            rhs_scale=x2_scales[:, c, :],
-                            start=(c == 0),
-                            stop=(c == PASSES - 1),
-                        )
-                nc.vector.scalar_tensor_tensor(
-                    out=x3_sb[:, s0 : s0 + 2, :],
-                    in0=spread[:],
-                    scalar=2.0,
-                    in1=x1_sb[:, s0 : s0 + 2, :],
-                    op0=ALU.mult,
-                    op1=ALU.subtract,
-                )
-            terms_of[b][3] = x3_sb
 
-        def pack(b):
-            xk_grouped = work.tile([P, SLOTS, PASSES, P, TERMS], BF16, align_bytes=64)
-            xk_codes = work.tile([P, SLOTS, PASSES, P], U32, align_bytes=64)
-            xk_scales = work.tile([P, SLOTS, PASSES, P], U8, align_bytes=64)
-            for s in range(SLOTS):
+        def diffuse(b, pair):
+            if pair == 0:
+                x3_sb = work.tile([P, SLOTS, FEATS], BF16)
+                terms_of[b][3] = x3_sb
+            x2_codes, x2_scales = x2_mx_of[b]
+            s0 = 2 * pair
+            spread = ps_diff.tile([P, 2, FEATS], F32)
+            for i in range(2):
+                for c in range(PASSES):
+                    nc.tensor.matmul_mx(
+                        out=spread[:, i, :],
+                        lhsT=adj_codes[:, s0 + i, c, :].bitcast(FP8X4),
+                        lhsT_scale=adj_scales[:, s0 + i, c, :],
+                        rhs=x2_codes[:, c, :].bitcast(FP8X4),
+                        rhs_scale=x2_scales[:, c, :],
+                        start=(c == 0),
+                        stop=(c == PASSES - 1),
+                    )
+            nc.vector.scalar_tensor_tensor(
+                out=terms_of[b][3][:, s0 : s0 + 2, :],
+                in0=spread[:],
+                scalar=2.0,
+                in1=terms_of[b][1][:, s0 : s0 + 2, :],
+                op0=ALU.mult,
+                op1=ALU.subtract,
+            )
+
+        def flip(b, pair):
+            for s in (2 * pair, 2 * pair + 1):
                 flipped = ps_flip.tile([P, PASSES, TERMS, P], BF16, tag="flip")
                 for c in range(PASSES):
                     for k in range(TERMS):
                         nc.tensor.transpose(
                             flipped[:, c, k, :], terms_of[b][k][:, s, c * P : (c + 1) * P], ident_bf[:]
                         )
+                flipped_of[(b, s)] = flipped
+
+        def gather(b, pair):
+            if pair == 0:
+                xk_grouped = work.tile([P, SLOTS, PASSES, P, TERMS], BF16, align_bytes=64)
+                xk_codes = work.tile([P, SLOTS, PASSES, P], U32, align_bytes=64)
+                xk_scales = work.tile([P, SLOTS, PASSES, P], U8, align_bytes=64)
+                xk_of[b] = (xk_grouped, xk_codes, xk_scales)
+            for s in (2 * pair, 2 * pair + 1):
                 copy = nc.vector.tensor_copy if s == SLOTS - 1 else nc.scalar.copy
-                copy(out=xk_grouped[:, s], in_=flipped[:].rearrange("f c k n -> f c n k"))
-                if s % 2 == 1:
-                    nc.vector.quantize_mx(
-                        out=xk_codes[:, s - 1 : s + 1].rearrange("f s c n -> f (s c n)").bitcast(FP8X4),
-                        scales=xk_scales[:, s - 1 : s + 1].rearrange("f s c n -> f (s c n)"),
-                        in_=xk_grouped[:, s - 1 : s + 1].rearrange("f s c n k -> f (s c n k)"),
+                copy(out=xk_of[b][0][:, s], in_=flipped_of[(b, s)][:].rearrange("f c k n -> f c n k"))
+
+        def quantise_xk(b, pair):
+            xk_grouped, xk_codes, xk_scales = xk_of[b]
+            s0 = 2 * pair
+            nc.vector.quantize_mx(
+                out=xk_codes[:, s0 : s0 + 2].rearrange("f s c n -> f (s c n)").bitcast(FP8X4),
+                scales=xk_scales[:, s0 : s0 + 2].rearrange("f s c n -> f (s c n)"),
+                in_=xk_grouped[:, s0 : s0 + 2].rearrange("f s c n k -> f (s c n k)"),
+            )
+
+        def multiply(b, pair):
+            xk_codes, xk_scales = xk_of[b][1], xk_of[b][2]
+            summed = ps_gate.tile([P, 2, GATES * UNITS], F32)
+            for i in range(2):
+                for c in range(PASSES):
+                    nc.tensor.matmul_mx(
+                        out=summed[:, i, :],
+                        lhsT=xk_codes[:, 2 * pair + i, c, :].bitcast(FP8X4),
+                        lhsT_scale=xk_scales[:, 2 * pair + i, c, :],
+                        rhs=w_codes[:, c, :].bitcast(FP8X4),
+                        rhs_scale=w_scales[:, c, :],
+                        start=(c == 0),
+                        stop=(c == PASSES - 1),
                     )
-            return xk_codes, xk_scales
+            summed_of[(b, pair)] = summed
 
-        def gates(b, xk_codes, xk_scales, h_sb):
-            result = outs.tile([P, GATES, SLOTS, UNITS], F32)
-            for s0 in range(0, SLOTS, 2):
-                summed = ps_gate.tile([P, 2, GATES * UNITS], F32)
-                for i in range(2):
-                    for c in range(PASSES):
-                        nc.tensor.matmul_mx(
-                            out=summed[:, i, :],
-                            lhsT=xk_codes[:, s0 + i, c, :].bitcast(FP8X4),
-                            lhsT_scale=xk_scales[:, s0 + i, c, :],
-                            rhs=w_codes[:, c, :].bitcast(FP8X4),
-                            rhs_scale=w_scales[:, c, :],
-                            start=(c == 0),
-                            stop=(c == PASSES - 1),
-                        )
-                biased = outs.tile([P, 2, GATES * UNITS], F32)
-                nc.vector.tensor_tensor(
-                    out=biased[:],
-                    in0=summed[:],
-                    in1=bias_bc[:].unsqueeze(1).to_broadcast([P, 2, GATES * UNITS]),
-                    op=ALU.add,
-                )
-                nc.scalar.activation(
-                    out=result[:, :, s0 : s0 + 2, :].rearrange("p g s j -> p s g j"),
-                    in_=biased[:].rearrange("p s (g j) -> p s g j", g=GATES),
-                    func=ACT.Sigmoid,
-                )
-            nc.gpsimd.tensor_tensor(out=result[:, 0], in0=result[:, 0], in1=h_sb[:], op=ALU.mult)
-            for gate, rows in enumerate((out_0[b], u_rows[b])):
-                nc.sync.dma_start(
-                    out=by_node(rows), in_=result[:, gate].rearrange("p (g t) j -> p g (t j)", g=PASSES)
-                )
+        def finish(b, pair):
+            if pair == 0:
+                result = outs.tile([P, GATES, SLOTS, UNITS], F32)
+                result_of[b] = result
+            result = result_of[b]
+            s0 = 2 * pair
+            biased = outs.tile([P, 2, GATES * UNITS], F32)
+            nc.vector.tensor_tensor(
+                out=biased[:],
+                in0=summed_of[(b, pair)][:],
+                in1=bias_bc[:].unsqueeze(1).to_broadcast([P, 2, GATES * UNITS]),
+                op=ALU.add,
+            )
+            nc.scalar.activation(
+                out=result[:, :, s0 : s0 + 2, :].rearrange("p g s j -> p s g j"),
+                in_=biased[:].rearrange("p s (g j) -> p s g j", g=GATES),
+                func=ACT.Sigmoid,
+            )
+            nc.gpsimd.tensor_tensor(
+                out=result[:, 0, s0 : s0 + 2, :],
+                in0=result[:, 0, s0 : s0 + 2, :],
+                in1=state_of[b][:, s0 : s0 + 2, :],
+                op=ALU.mult,
+            )
+            if pair % 2 == 1:
+                g = pair // 2
+                for gate in range(GATES):
+                    nc.sync.dma_start(
+                        out=by_node(out_rows[gate][b])[:, g, :],
+                        in_=result[:, gate, g * PACK : (g + 1) * PACK, :].rearrange("p t j -> p (t j)"),
+                    )
 
-        packed_of = {}
-        state_of = {}
-        for step in range(BATCH + 2):
-            if step + 2 < BATCH:
-                terms_of[step + 2] = load_terms(step + 2)
-            if step < BATCH:
-                state_of[step] = load_state(step)
-                diffuse(step)
-            if 1 <= step <= BATCH:
-                packed_of[step - 1] = pack(step - 1)
-            if step >= 2:
-                codes, scales = packed_of[step - 2]
-                gates(step - 2, codes, scales, state_of[step - 2])
+        pairs = SLOTS // 2
+        ticks = BATCH * pairs
+        for tick in range(ticks + 4):
+            if tick % pairs == 0 and tick // pairs + 2 < BATCH:
+                load_batch(tick // pairs + 2)
+            if 3 <= tick < ticks + 3:
+                quantise_xk(*divmod(tick - 3, pairs))
+            if tick < ticks:
+                diffuse(*divmod(tick, pairs))
+            if 1 <= tick < ticks + 1:
+                flip(*divmod(tick - 1, pairs))
+            if 2 <= tick < ticks + 2:
+                gather(*divmod(tick - 2, pairs))
+            if tick == 2:
+                quantise_kernels()
+            if 3 <= tick < ticks + 3:
+                multiply(*divmod(tick - 3, pairs))
+            if 4 <= tick:
+                finish(*divmod(tick - 4, pairs))
+            if tick % pairs == 1 and tick // pairs + 1 < BATCH:
+                quantise_x2(tick // pairs + 1)

@@ -41,7 +41,6 @@ def tile_gts_gcgrucell_pb_t_kernel(
         ps_flip = ctx.enter_context(tc.psum_pool(name="ps_flip", bufs=4))
         ps_diff = ctx.enter_context(tc.psum_pool(name="ps_diff", bufs=2))
         ps_gate = ctx.enter_context(tc.psum_pool(name="ps_gate", bufs=2))
-        ctx.enter_context(tc.manual_schedule())
 
         x_dram = [x0, x1, x2]
         h_rows = h_prev.rearrange("b (n j) -> b n j", j=UNITS)

@@ -21,6 +21,9 @@ TERMS = 4
 PASSES = 2
 SLOTS = NODES // P
 GATES = 2
+RUN = 8
+CLASSES = 4
+STRETCHES = FEATS // (RUN * CLASSES)
 
 FLOPS = 2 * BATCH * NODES * NODES * FEATS + 2 * BATCH * NODES * (TERMS * FEATS) * (GATES * UNITS)
 
@@ -35,7 +38,9 @@ def tile_gts_gcgrucell_pb_t_kernel(
     nc = tc.nc
     with ExitStack() as ctx:
         const = ctx.enter_context(tc.tile_pool(name="const", bufs=1))
-        loads = ctx.enter_context(tc.tile_pool(name="loads", bufs=4))
+        loads = ctx.enter_context(tc.tile_pool(name="loads", bufs=2))
+        states = ctx.enter_context(tc.tile_pool(name="states", bufs=4))
+        terms = ctx.enter_context(tc.tile_pool(name="terms", bufs=3))
         work = ctx.enter_context(tc.tile_pool(name="work", bufs=2))
         outs = ctx.enter_context(tc.tile_pool(name="outs", bufs=3))
         ps_flip = ctx.enter_context(tc.psum_pool(name="ps_flip", bufs=4))
@@ -46,8 +51,10 @@ def tile_gts_gcgrucell_pb_t_kernel(
         h_rows = h_prev.rearrange("b (n j) -> b n j", j=UNITS)
         out_rows = [out_0, out_1.rearrange("b (n j) -> b n j", j=UNITS)]
 
+        loaded_of = {}
         terms_of = {}
         state_of = {}
+        x2_grouped_of = {}
         x2_mx_of = {}
         flipped_of = {}
         xk_of = {}
@@ -55,39 +62,58 @@ def tile_gts_gcgrucell_pb_t_kernel(
         result_of = {}
 
         def load_term(b, k):
-            x_sb = loads.tile([P, SLOTS, FEATS], BF16, name="x%d_sb" % k)
+            x_raw = loads.tile([P, SLOTS, FEATS], BF16, name="x%d_raw" % k)
             nc.sync.dma_start(
-                out=x_sb[:].rearrange("p (g t) f -> p g (t f)", g=PASSES), in_=by_node(x_dram[k][b])
+                out=x_raw[:].rearrange("p (g t) f -> p g (t f)", g=PASSES), in_=by_node(x_dram[k][b])
             )
-            terms_of[b][k] = x_sb
+            loaded_of[b][k] = x_raw
 
-        def load_batch(b):
-            terms_of[b] = {}
-            for k in (2, 1, 0):
-                load_term(b, k)
-            h_sb = loads.tile([P, SLOTS, UNITS], BF16)
+        def load_state(b):
+            h_sb = states.tile([P, SLOTS, UNITS], BF16)
             nc.sync.dma_start(
                 out=h_sb[:].rearrange("p (g t) j -> p g (t j)", g=PASSES), in_=by_node(h_rows[b])
             )
             state_of[b] = h_sb
 
-        def quantise_x2(b):
+        def load_batch(b):
+            loaded_of[b] = {}
+            terms_of[b] = {}
+            for k in (2, 1, 0):
+                load_term(b, k)
+            load_state(b)
+
+        def place_features(b, k):
+            x_raw = loaded_of[b][k]
+            x_sb = terms.tile([P, SLOTS, FEATS], BF16, name="x%d_sb" % k)
+            width = RUN * STRETCHES
+            for c in range(CLASSES):
+                nc.vector.tensor_copy(
+                    out=x_sb[:, :, c * width : (c + 1) * width].rearrange("p s (j i) -> p s j i", i=RUN),
+                    in_=x_raw[:].rearrange("p s (j c i) -> p c s j i", c=CLASSES, i=RUN)[:, c],
+                )
+            terms_of[b][k] = x_sb
+
+        def group_x2(b):
             x2_sb = terms_of[b][2]
             x2_grouped = work.tile([P, PASSES, FEATS, PACK], BF16, align_bytes=64)
             for g in range(PASSES):
-                nc.vector.tensor_copy(
+                nc.scalar.copy(
                     out=x2_grouped[:, g].rearrange("p (c i) t -> p c t i", i=4),
                     in_=x2_sb[:, g * PACK : (g + 1) * PACK, :].rearrange("p t (c i) -> p c t i", i=4),
                 )
+            x2_grouped_of[b] = x2_grouped
+
+        def quantise_x2(b):
             x2_codes = work.tile([P, PASSES, FEATS], U32, align_bytes=64)
             x2_scales = work.tile([P, PASSES, FEATS], U8, align_bytes=64)
             nc.vector.quantize_mx(
                 out=x2_codes[:].rearrange("p g f -> p (g f)").bitcast(FP8X4),
                 scales=x2_scales[:].rearrange("p g f -> p (g f)"),
-                in_=x2_grouped[:].rearrange("p g f t -> p (g f t)"),
+                in_=x2_grouped_of[b][:].rearrange("p g f t -> p (g f t)"),
             )
             x2_mx_of[b] = (x2_codes, x2_scales)
 
+        loaded_of[0] = {}
         terms_of[0] = {}
         load_term(0, 2)
         adj_sb = const.tile([P, PASSES, PACK * NODES], BF16)
@@ -95,20 +121,14 @@ def tile_gts_gcgrucell_pb_t_kernel(
             nc.sync.dma_start(out=adj_sb[:, g, :], in_=by_node(adj)[:, g, :])
         load_term(0, 1)
         load_term(0, 0)
-        w_raw = const.tile([P, GATES, PASSES, PACK, UNITS], BF16)
+        rows_here = TERMS * FEATS // P
+        w_raw = const.tile([P, GATES, rows_here * UNITS], BF16)
         for gate, kernel in enumerate((r_kernel, u_kernel)):
-            nc.sync.dma_start(
-                out=w_raw[:, gate].rearrange("p c t j -> p c (t j)"),
-                in_=kernel.rearrange("(c p t) j -> p c (t j)", c=PASSES, p=P, t=PACK),
-            )
+            nc.sync.dma_start(out=w_raw[:, gate, :], in_=kernel.rearrange("(p r) j -> p (r j)", p=P))
         bias_bc = const.tile([P, GATES * UNITS], BF16)
         nc.sync.dma_start(out=bias_bc[:, 0:UNITS], in_=r_bias.partition_broadcast(P))
         nc.sync.dma_start(out=bias_bc[:, UNITS : 2 * UNITS], in_=u_bias.partition_broadcast(P))
-        h0_sb = loads.tile([P, SLOTS, UNITS], BF16, name="h_sb")
-        nc.sync.dma_start(
-            out=h0_sb[:].rearrange("p (g t) j -> p g (t j)", g=PASSES), in_=by_node(h_rows[0])
-        )
-        state_of[0] = h0_sb
+        load_state(0)
         load_batch(1)
 
         ident_f32 = const.tile([P, P], F32)
@@ -116,6 +136,8 @@ def tile_gts_gcgrucell_pb_t_kernel(
         ident_bf = const.tile([P, P], BF16)
         make_identity(nc, ident_bf[:])
 
+        place_features(0, 2)
+        group_x2(0)
         quantise_x2(0)
 
         adj_words = adj_sb[:].rearrange("p g w -> p (g w)").bitcast(F32).rearrange(
@@ -142,15 +164,34 @@ def tile_gts_gcgrucell_pb_t_kernel(
                     in_=adj_grouped[:, (s - 1) * slot_cols : (s + 1) * slot_cols],
                 )
 
+        place_features(0, 1)
+        place_features(0, 0)
+
+        shuffle = const.tile([P, P], BF16)
+        nc.vector.tensor_copy(
+            out=shuffle[:].rearrange("k (c j i) -> k c j i", c=CLASSES, j=STRETCHES),
+            in_=ident_bf[:].rearrange("k (j c i) -> k c j i", c=CLASSES, j=STRETCHES),
+        )
         w_grouped = const.tile([P, PASSES, GATES, UNITS, PACK], BF16, align_bytes=64)
         w_codes = const.tile([P, PASSES, GATES * UNITS], U32, align_bytes=64)
         w_scales = const.tile([P, PASSES, GATES * UNITS], U8, align_bytes=64)
 
         def quantise_kernels():
-            for c in range(PASSES):
-                for gate in range(GATES):
-                    nc.vector.tensor_copy(
-                        out=w_grouped[:, c, gate], in_=w_raw[:, gate, c].rearrange("p t j -> p j t")
+            half = rows_here * UNITS // 2
+            for gate in range(GATES):
+                w_moved = ps_flip.tile([P, rows_here * UNITS], BF16, tag="flip")
+                for i in range(2):
+                    nc.tensor.matmul(
+                        out=w_moved[:, i * half : (i + 1) * half],
+                        lhsT=shuffle[:],
+                        rhs=w_raw[:, gate, i * half : (i + 1) * half],
+                        start=True,
+                        stop=True,
+                    )
+                for a in range(PASSES):
+                    nc.scalar.copy(
+                        out=w_grouped[:, a, gate].rearrange("w j (u e) -> w j u e", e=2),
+                        in_=w_moved[:].rearrange("w (e a u j) -> w a j u e", e=2, a=PASSES, u=2)[:, a],
                     )
             nc.vector.quantize_mx(
                 out=w_codes[:].rearrange("p c j -> p (c j)").bitcast(FP8X4),
@@ -160,7 +201,7 @@ def tile_gts_gcgrucell_pb_t_kernel(
 
         def diffuse(b, pair):
             if pair == 0:
-                x3_sb = work.tile([P, SLOTS, FEATS], BF16)
+                x3_sb = terms.tile([P, SLOTS, FEATS], BF16, name="x3_sb")
                 terms_of[b][3] = x3_sb
             x2_codes, x2_scales = x2_mx_of[b]
             s0 = 2 * pair
@@ -187,23 +228,24 @@ def tile_gts_gcgrucell_pb_t_kernel(
 
         def flip(b, pair):
             for s in (2 * pair, 2 * pair + 1):
-                flipped = ps_flip.tile([P, PASSES, TERMS, P], BF16, tag="flip")
-                for c in range(PASSES):
-                    for k in range(TERMS):
-                        nc.tensor.transpose(
-                            flipped[:, c, k, :], terms_of[b][k][:, s, c * P : (c + 1) * P], ident_bf[:]
-                        )
+                flipped = ps_flip.tile([P, TERMS, P], F32, tag="flip")
+                for k in range(TERMS):
+                    nc.tensor.transpose(flipped[:, k, :], terms_of[b][k][:, s, :].bitcast(F32), ident_f32[:])
                 flipped_of[(b, s)] = flipped
 
         def gather(b, pair):
             if pair == 0:
-                xk_grouped = work.tile([P, SLOTS, PASSES, P, TERMS], BF16, align_bytes=64)
+                xk_grouped = work.tile([P, SLOTS * slot_cols], BF16, align_bytes=64)
                 xk_codes = work.tile([P, SLOTS, PASSES, P], U32, align_bytes=64)
                 xk_scales = work.tile([P, SLOTS, PASSES, P], U8, align_bytes=64)
                 xk_of[b] = (xk_grouped, xk_codes, xk_scales)
+            xk_words = xk_of[b][0][:].bitcast(F32).rearrange(
+                "w (s a n u) -> w s a n u", s=SLOTS, a=PASSES, n=P, u=2
+            )
             for s in (2 * pair, 2 * pair + 1):
-                copy = nc.vector.tensor_copy if s == SLOTS - 1 else nc.scalar.copy
-                copy(out=xk_of[b][0][:, s], in_=flipped_of[(b, s)][:].rearrange("f c k n -> f c n k"))
+                nc.scalar.copy(
+                    out=xk_words[:, s], in_=flipped_of[(b, s)][:].rearrange("w (a u) n -> w a n u", a=PASSES)
+                )
 
         def quantise_xk(b, pair):
             xk_grouped, xk_codes, xk_scales = xk_of[b]
@@ -211,7 +253,7 @@ def tile_gts_gcgrucell_pb_t_kernel(
             nc.vector.quantize_mx(
                 out=xk_codes[:, s0 : s0 + 2].rearrange("f s c n -> f (s c n)").bitcast(FP8X4),
                 scales=xk_scales[:, s0 : s0 + 2].rearrange("f s c n -> f (s c n)"),
-                in_=xk_grouped[:, s0 : s0 + 2].rearrange("f s c n k -> f (s c n k)"),
+                in_=xk_grouped[:, s0 * slot_cols : (s0 + 2) * slot_cols],
             )
 
         def multiply(b, pair):
@@ -265,8 +307,9 @@ def tile_gts_gcgrucell_pb_t_kernel(
         pairs = SLOTS // 2
         ticks = BATCH * pairs
         for tick in range(ticks + 4):
-            if tick % pairs == 0 and tick // pairs + 2 < BATCH:
-                load_batch(tick // pairs + 2)
+            ahead = tick // pairs + 1
+            if tick % pairs == 0 and ahead + 1 < BATCH:
+                load_batch(ahead + 1)
             if 3 <= tick < ticks + 3:
                 quantise_xk(*divmod(tick - 3, pairs))
             if tick < ticks:
@@ -281,5 +324,12 @@ def tile_gts_gcgrucell_pb_t_kernel(
                 multiply(*divmod(tick - 3, pairs))
             if 4 <= tick:
                 finish(*divmod(tick - 4, pairs))
-            if tick % pairs == 1 and tick // pairs + 1 < BATCH:
-                quantise_x2(tick // pairs + 1)
+            if ahead < BATCH:
+                if tick % pairs == 0:
+                    place_features(ahead, 2)
+                if tick % pairs == 1:
+                    group_x2(ahead)
+                    place_features(ahead, 1)
+                if tick % pairs == 2:
+                    quantise_x2(ahead)
+                    place_features(ahead, 0)

@@ -24,6 +24,7 @@ GATES = 2
 RUN = 8
 CLASSES = 4
 STRETCHES = FEATS // (RUN * CLASSES)
+LEAD = 3
 
 FLOPS = 2 * BATCH * NODES * NODES * FEATS + 2 * BATCH * NODES * (TERMS * FEATS) * (GATES * UNITS)
 
@@ -39,9 +40,11 @@ def tile_gts_gcgrucell_pb_t_kernel(
     with ExitStack() as ctx:
         const = ctx.enter_context(tc.tile_pool(name="const", bufs=1))
         loads = ctx.enter_context(tc.tile_pool(name="loads", bufs=2))
-        states = ctx.enter_context(tc.tile_pool(name="states", bufs=4))
-        terms = ctx.enter_context(tc.tile_pool(name="terms", bufs=3))
+        states = ctx.enter_context(tc.tile_pool(name="states", bufs=LEAD + 3))
+        terms = ctx.enter_context(tc.tile_pool(name="terms", bufs=LEAD + 2))
+        spread_out = ctx.enter_context(tc.tile_pool(name="spread_out", bufs=3))
         work = ctx.enter_context(tc.tile_pool(name="work", bufs=2))
+        pairs_pool = ctx.enter_context(tc.tile_pool(name="pairs_pool", bufs=3))
         outs = ctx.enter_context(tc.tile_pool(name="outs", bufs=3))
         ps_flip = ctx.enter_context(tc.psum_pool(name="ps_flip", bufs=4))
         ps_diff = ctx.enter_context(tc.psum_pool(name="ps_diff", bufs=2))
@@ -85,12 +88,10 @@ def tile_gts_gcgrucell_pb_t_kernel(
         def place_features(b, k):
             x_raw = loaded_of[b][k]
             x_sb = terms.tile([P, SLOTS, FEATS], BF16, name="x%d_sb" % k)
-            width = RUN * STRETCHES
-            for c in range(CLASSES):
-                nc.vector.tensor_copy(
-                    out=x_sb[:, :, c * width : (c + 1) * width].rearrange("p s (j i) -> p s j i", i=RUN),
-                    in_=x_raw[:].rearrange("p s (j c i) -> p c s j i", c=CLASSES, i=RUN)[:, c],
-                )
+            nc.vector.tensor_copy(
+                out=x_sb[:].rearrange("p s (c j i) -> p c s j i", c=CLASSES, i=RUN),
+                in_=x_raw[:].rearrange("p s (j c i) -> p c s j i", c=CLASSES, i=RUN),
+            )
             terms_of[b][k] = x_sb
 
         def group_x2(b):
@@ -104,8 +105,8 @@ def tile_gts_gcgrucell_pb_t_kernel(
             x2_grouped_of[b] = x2_grouped
 
         def quantise_x2(b):
-            x2_codes = work.tile([P, PASSES, FEATS], U32, align_bytes=64)
-            x2_scales = work.tile([P, PASSES, FEATS], U8, align_bytes=64)
+            x2_codes = terms.tile([P, PASSES, FEATS], U32, align_bytes=64)
+            x2_scales = terms.tile([P, PASSES, FEATS], U8, align_bytes=64)
             nc.vector.quantize_mx(
                 out=x2_codes[:].rearrange("p g f -> p (g f)").bitcast(FP8X4),
                 scales=x2_scales[:].rearrange("p g f -> p (g f)"),
@@ -115,16 +116,24 @@ def tile_gts_gcgrucell_pb_t_kernel(
 
         loaded_of[0] = {}
         terms_of[0] = {}
-        load_term(0, 2)
         adj_sb = const.tile([P, PASSES, PACK * NODES], BF16)
-        for g in range(PASSES):
-            nc.sync.dma_start(out=adj_sb[:, g, :], in_=by_node(adj)[:, g, :])
+
+        def load_adj(pair):
+            g, i = divmod(pair, 2)
+            cols = slice(i * 2 * NODES, (i + 1) * 2 * NODES)
+            nc.sync.dma_start(out=adj_sb[:, g, cols], in_=by_node(adj)[:, g, cols])
+
+        load_term(0, 2)
+        load_adj(0)
+        load_adj(1)
         load_term(0, 1)
-        load_term(0, 0)
         rows_here = TERMS * FEATS // P
         w_raw = const.tile([P, GATES, rows_here * UNITS], BF16)
         for gate, kernel in enumerate((r_kernel, u_kernel)):
             nc.sync.dma_start(out=w_raw[:, gate, :], in_=kernel.rearrange("(p r) j -> p (r j)", p=P))
+        load_term(0, 0)
+        load_adj(2)
+        load_adj(3)
         bias_bc = const.tile([P, GATES * UNITS], BF16)
         nc.sync.dma_start(out=bias_bc[:, 0:UNITS], in_=r_bias.partition_broadcast(P))
         nc.sync.dma_start(out=bias_bc[:, UNITS : 2 * UNITS], in_=u_bias.partition_broadcast(P))
@@ -150,20 +159,24 @@ def tile_gts_gcgrucell_pb_t_kernel(
         adj_codes = const.tile([P, SLOTS, PASSES, P], U32, align_bytes=64)
         adj_scales = const.tile([P, SLOTS, PASSES, P], U8, align_bytes=64)
         slot_cols = PASSES * P * PACK
-        for s in range(SLOTS):
-            adj_flipped = ps_flip.tile([P, PASSES, 2, P], F32, tag="flip")
-            for c in range(PASSES):
-                for u in range(2):
-                    nc.tensor.transpose(adj_flipped[:, c, u, :], adj_words[:, s, c, u, :], ident_f32[:])
-            copy = nc.vector.tensor_copy if s % 2 == 0 else nc.scalar.copy
-            copy(out=adj_grouped_words[:, s], in_=adj_flipped[:].rearrange("q c u n -> q c n u"))
-            if s % 2 == 1:
-                nc.vector.quantize_mx(
-                    out=adj_codes[:, s - 1 : s + 1].rearrange("q s c n -> q (s c n)").bitcast(FP8X4),
-                    scales=adj_scales[:, s - 1 : s + 1].rearrange("q s c n -> q (s c n)"),
-                    in_=adj_grouped[:, (s - 1) * slot_cols : (s + 1) * slot_cols],
-                )
 
+        def quantise_adj(pair):
+            for s in (2 * pair, 2 * pair + 1):
+                adj_flipped = ps_flip.tile([P, PASSES, 2, P], F32, tag="flip")
+                for c in range(PASSES):
+                    for u in range(2):
+                        nc.tensor.transpose(adj_flipped[:, c, u, :], adj_words[:, s, c, u, :], ident_f32[:])
+                copy = nc.vector.tensor_copy if s % 2 == 0 else nc.scalar.copy
+                copy(out=adj_grouped_words[:, s], in_=adj_flipped[:].rearrange("q c u n -> q c n u"))
+            s0 = 2 * pair
+            nc.vector.quantize_mx(
+                out=adj_codes[:, s0 : s0 + 2].rearrange("q s c n -> q (s c n)").bitcast(FP8X4),
+                scales=adj_scales[:, s0 : s0 + 2].rearrange("q s c n -> q (s c n)"),
+                in_=adj_grouped[:, s0 * slot_cols : (s0 + 2) * slot_cols],
+            )
+
+        quantise_adj(0)
+        quantise_adj(1)
         place_features(0, 1)
         place_features(0, 0)
 
@@ -199,9 +212,12 @@ def tile_gts_gcgrucell_pb_t_kernel(
                 in_=w_grouped[:].rearrange("p c g j t -> p (c g j t)"),
             )
 
+        quantise_kernels()
+
+
         def diffuse(b, pair):
             if pair == 0:
-                x3_sb = terms.tile([P, SLOTS, FEATS], BF16, name="x3_sb")
+                x3_sb = spread_out.tile([P, SLOTS, FEATS], BF16)
                 terms_of[b][3] = x3_sb
             x2_codes, x2_scales = x2_mx_of[b]
             s0 = 2 * pair
@@ -234,37 +250,34 @@ def tile_gts_gcgrucell_pb_t_kernel(
                 flipped_of[(b, s)] = flipped
 
         def gather(b, pair):
-            if pair == 0:
-                xk_grouped = work.tile([P, SLOTS * slot_cols], BF16, align_bytes=64)
-                xk_codes = work.tile([P, SLOTS, PASSES, P], U32, align_bytes=64)
-                xk_scales = work.tile([P, SLOTS, PASSES, P], U8, align_bytes=64)
-                xk_of[b] = (xk_grouped, xk_codes, xk_scales)
-            xk_words = xk_of[b][0][:].bitcast(F32).rearrange(
-                "w (s a n u) -> w s a n u", s=SLOTS, a=PASSES, n=P, u=2
-            )
-            for s in (2 * pair, 2 * pair + 1):
+            xk_grouped = pairs_pool.tile([P, 2 * slot_cols], BF16, align_bytes=64)
+            xk_codes = pairs_pool.tile([P, 2, PASSES, P], U32, align_bytes=64)
+            xk_scales = pairs_pool.tile([P, 2, PASSES, P], U8, align_bytes=64)
+            xk_of[(b, pair)] = (xk_grouped, xk_codes, xk_scales)
+            xk_words = xk_grouped[:].bitcast(F32).rearrange("w (s a n u) -> w s a n u", s=2, a=PASSES, n=P, u=2)
+            for i in range(2):
                 nc.scalar.copy(
-                    out=xk_words[:, s], in_=flipped_of[(b, s)][:].rearrange("w (a u) n -> w a n u", a=PASSES)
+                    out=xk_words[:, i],
+                    in_=flipped_of[(b, 2 * pair + i)][:].rearrange("w (a u) n -> w a n u", a=PASSES),
                 )
 
         def quantise_xk(b, pair):
-            xk_grouped, xk_codes, xk_scales = xk_of[b]
-            s0 = 2 * pair
+            xk_grouped, xk_codes, xk_scales = xk_of[(b, pair)]
             nc.vector.quantize_mx(
-                out=xk_codes[:, s0 : s0 + 2].rearrange("f s c n -> f (s c n)").bitcast(FP8X4),
-                scales=xk_scales[:, s0 : s0 + 2].rearrange("f s c n -> f (s c n)"),
-                in_=xk_grouped[:, s0 * slot_cols : (s0 + 2) * slot_cols],
+                out=xk_codes[:].rearrange("f s c n -> f (s c n)").bitcast(FP8X4),
+                scales=xk_scales[:].rearrange("f s c n -> f (s c n)"),
+                in_=xk_grouped[:],
             )
 
         def multiply(b, pair):
-            xk_codes, xk_scales = xk_of[b][1], xk_of[b][2]
+            xk_codes, xk_scales = xk_of[(b, pair)][1], xk_of[(b, pair)][2]
             summed = ps_gate.tile([P, 2, GATES * UNITS], F32)
             for i in range(2):
                 for c in range(PASSES):
                     nc.tensor.matmul_mx(
                         out=summed[:, i, :],
-                        lhsT=xk_codes[:, 2 * pair + i, c, :].bitcast(FP8X4),
-                        lhsT_scale=xk_scales[:, 2 * pair + i, c, :],
+                        lhsT=xk_codes[:, i, c, :].bitcast(FP8X4),
+                        lhsT_scale=xk_scales[:, i, c, :],
                         rhs=w_codes[:, c, :].bitcast(FP8X4),
                         rhs_scale=w_scales[:, c, :],
                         start=(c == 0),
@@ -273,11 +286,12 @@ def tile_gts_gcgrucell_pb_t_kernel(
             summed_of[(b, pair)] = summed
 
         def finish(b, pair):
-            if pair == 0:
-                result = outs.tile([P, GATES, SLOTS, UNITS], F32)
+            if pair % 2 == 0:
+                result = outs.tile([P, GATES, PACK, UNITS], F32)
                 result_of[b] = result
             result = result_of[b]
             s0 = 2 * pair
+            i0 = s0 % PACK
             biased = outs.tile([P, 2, GATES * UNITS], F32)
             nc.vector.tensor_tensor(
                 out=biased[:],
@@ -286,13 +300,13 @@ def tile_gts_gcgrucell_pb_t_kernel(
                 op=ALU.add,
             )
             nc.scalar.activation(
-                out=result[:, :, s0 : s0 + 2, :].rearrange("p g s j -> p s g j"),
+                out=result[:, :, i0 : i0 + 2, :].rearrange("p g s j -> p s g j"),
                 in_=biased[:].rearrange("p s (g j) -> p s g j", g=GATES),
                 func=ACT.Sigmoid,
             )
             nc.gpsimd.tensor_tensor(
-                out=result[:, 0, s0 : s0 + 2, :],
-                in0=result[:, 0, s0 : s0 + 2, :],
+                out=result[:, 0, i0 : i0 + 2, :],
+                in0=result[:, 0, i0 : i0 + 2, :],
                 in1=state_of[b][:, s0 : s0 + 2, :],
                 op=ALU.mult,
             )
@@ -301,7 +315,7 @@ def tile_gts_gcgrucell_pb_t_kernel(
                 for gate in range(GATES):
                     nc.sync.dma_start(
                         out=by_node(out_rows[gate][b])[:, g, :],
-                        in_=result[:, gate, g * PACK : (g + 1) * PACK, :].rearrange("p t j -> p (t j)"),
+                        in_=result[:, gate].rearrange("p t j -> p (t j)"),
                     )
 
         pairs = SLOTS // 2
@@ -314,12 +328,12 @@ def tile_gts_gcgrucell_pb_t_kernel(
                 quantise_xk(*divmod(tick - 3, pairs))
             if tick < ticks:
                 diffuse(*divmod(tick, pairs))
+            if tick < 2:
+                quantise_adj(tick + 2)
             if 1 <= tick < ticks + 1:
                 flip(*divmod(tick - 1, pairs))
             if 2 <= tick < ticks + 2:
                 gather(*divmod(tick - 2, pairs))
-            if tick == 2:
-                quantise_kernels()
             if 3 <= tick < ticks + 3:
                 multiply(*divmod(tick - 3, pairs))
             if 4 <= tick:

@@ -134,9 +134,10 @@ def tile_gts_gcgrucell_pb_t_kernel(
         load_term(0, 0)
         load_adj(2)
         load_adj(3)
-        bias_bc = const.tile([P, GATES * UNITS], BF16)
-        nc.sync.dma_start(out=bias_bc[:, 0:UNITS], in_=r_bias.partition_broadcast(P))
-        nc.sync.dma_start(out=bias_bc[:, UNITS : 2 * UNITS], in_=u_bias.partition_broadcast(P))
+        bias_row = const.tile([P, GATES * UNITS], BF16)
+        nc.gpsimd.memset(bias_row[:], 0.0)
+        nc.sync.dma_start(out=bias_row[0:1, 0:UNITS], in_=r_bias.rearrange("(o j) -> o j", o=1))
+        nc.sync.dma_start(out=bias_row[0:1, UNITS : 2 * UNITS], in_=u_bias.rearrange("(o j) -> o j", o=1))
         load_state(0)
         load_batch(1)
 
@@ -213,6 +214,13 @@ def tile_gts_gcgrucell_pb_t_kernel(
             )
 
         quantise_kernels()
+
+        ones = const.tile([P, P], BF16)
+        nc.gpsimd.memset(ones[:], 1.0)
+        bias_sum = ps_gate.tile([P, 2, GATES * UNITS], F32, tag="summed")
+        nc.tensor.matmul(out=bias_sum[:, 0, :], lhsT=ones[:], rhs=bias_row[:], start=True, stop=True)
+        bias_bc = const.tile([P, GATES * UNITS], F32)
+        nc.scalar.copy(out=bias_bc[:], in_=bias_sum[:, 0, :])
 
 
         def diffuse(b, pair):

@@ -118,22 +118,23 @@ def tile_gts_gcgrucell_pb_t_kernel(
         terms_of[0] = {}
         adj_sb = const.tile([P, PASSES, PACK * NODES], BF16)
 
-        def load_adj(pair):
-            g, i = divmod(pair, 2)
-            cols = slice(i * 2 * NODES, (i + 1) * 2 * NODES)
+        def load_adj(s0, n):
+            g, t = divmod(s0, PACK)
+            cols = slice(t * NODES, (t + n) * NODES)
             nc.sync.dma_start(out=adj_sb[:, g, cols], in_=by_node(adj)[:, g, cols])
 
         load_term(0, 2)
-        load_adj(0)
-        load_adj(1)
+        load_adj(0, 1)
+        load_adj(1, 1)
+        load_adj(2, 2)
         load_term(0, 1)
         rows_here = TERMS * FEATS // P
         w_raw = const.tile([P, GATES, rows_here * UNITS], BF16)
         for gate, kernel in enumerate((r_kernel, u_kernel)):
             nc.sync.dma_start(out=w_raw[:, gate, :], in_=kernel.rearrange("(p r) j -> p (r j)", p=P))
         load_term(0, 0)
-        load_adj(2)
-        load_adj(3)
+        load_adj(4, 2)
+        load_adj(6, 2)
         bias_row = const.tile([P, GATES * UNITS], BF16)
         nc.gpsimd.memset(bias_row[:], 0.0)
         nc.sync.dma_start(out=bias_row[0:1, 0:UNITS], in_=r_bias.rearrange("(o j) -> o j", o=1))
@@ -161,23 +162,23 @@ def tile_gts_gcgrucell_pb_t_kernel(
         adj_scales = const.tile([P, SLOTS, PASSES, P], U8, align_bytes=64)
         slot_cols = PASSES * P * PACK
 
-        def quantise_adj(pair):
-            for s in (2 * pair, 2 * pair + 1):
+        def quantise_adj(s0, n):
+            for s in range(s0, s0 + n):
                 adj_flipped = ps_flip.tile([P, PASSES, 2, P], F32, tag="flip")
                 for c in range(PASSES):
                     for u in range(2):
                         nc.tensor.transpose(adj_flipped[:, c, u, :], adj_words[:, s, c, u, :], ident_f32[:])
                 copy = nc.vector.tensor_copy if s % 2 == 0 else nc.scalar.copy
                 copy(out=adj_grouped_words[:, s], in_=adj_flipped[:].rearrange("q c u n -> q c n u"))
-            s0 = 2 * pair
             nc.vector.quantize_mx(
-                out=adj_codes[:, s0 : s0 + 2].rearrange("q s c n -> q (s c n)").bitcast(FP8X4),
-                scales=adj_scales[:, s0 : s0 + 2].rearrange("q s c n -> q (s c n)"),
-                in_=adj_grouped[:, s0 * slot_cols : (s0 + 2) * slot_cols],
+                out=adj_codes[:, s0 : s0 + n].rearrange("q s c n -> q (s c n)").bitcast(FP8X4),
+                scales=adj_scales[:, s0 : s0 + n].rearrange("q s c n -> q (s c n)"),
+                in_=adj_grouped[:, s0 * slot_cols : (s0 + n) * slot_cols],
             )
 
-        quantise_adj(0)
-        quantise_adj(1)
+        quantise_adj(0, 1)
+        quantise_adj(1, 1)
+        quantise_adj(2, 2)
         place_features(0, 1)
         place_features(0, 0)
 
@@ -223,14 +224,13 @@ def tile_gts_gcgrucell_pb_t_kernel(
         nc.scalar.copy(out=bias_bc[:], in_=bias_sum[:, 0, :])
 
 
-        def diffuse(b, pair):
-            if pair == 0:
+        def diffuse(b, s0, n):
+            if s0 == 0:
                 x3_sb = spread_out.tile([P, SLOTS, FEATS], BF16)
                 terms_of[b][3] = x3_sb
             x2_codes, x2_scales = x2_mx_of[b]
-            s0 = 2 * pair
             spread = ps_diff.tile([P, 2, FEATS], F32)
-            for i in range(2):
+            for i in range(n):
                 for c in range(PASSES):
                     nc.tensor.matmul_mx(
                         out=spread[:, i, :],
@@ -242,45 +242,45 @@ def tile_gts_gcgrucell_pb_t_kernel(
                         stop=(c == PASSES - 1),
                     )
             nc.vector.scalar_tensor_tensor(
-                out=terms_of[b][3][:, s0 : s0 + 2, :],
-                in0=spread[:],
+                out=terms_of[b][3][:, s0 : s0 + n, :],
+                in0=spread[:, 0:n, :],
                 scalar=2.0,
-                in1=terms_of[b][1][:, s0 : s0 + 2, :],
+                in1=terms_of[b][1][:, s0 : s0 + n, :],
                 op0=ALU.mult,
                 op1=ALU.subtract,
             )
 
-        def flip(b, pair):
-            for s in (2 * pair, 2 * pair + 1):
+        def flip(b, s0, n):
+            for s in range(s0, s0 + n):
                 flipped = ps_flip.tile([P, TERMS, P], F32, tag="flip")
                 for k in range(TERMS):
                     nc.tensor.transpose(flipped[:, k, :], terms_of[b][k][:, s, :].bitcast(F32), ident_f32[:])
                 flipped_of[(b, s)] = flipped
 
-        def gather(b, pair):
+        def gather(b, s0, n):
             xk_grouped = pairs_pool.tile([P, 2 * slot_cols], BF16, align_bytes=64)
             xk_codes = pairs_pool.tile([P, 2, PASSES, P], U32, align_bytes=64)
             xk_scales = pairs_pool.tile([P, 2, PASSES, P], U8, align_bytes=64)
-            xk_of[(b, pair)] = (xk_grouped, xk_codes, xk_scales)
+            xk_of[(b, s0)] = (xk_grouped, xk_codes, xk_scales)
             xk_words = xk_grouped[:].bitcast(F32).rearrange("w (s a n u) -> w s a n u", s=2, a=PASSES, n=P, u=2)
-            for i in range(2):
+            for i in range(n):
                 nc.scalar.copy(
                     out=xk_words[:, i],
-                    in_=flipped_of[(b, 2 * pair + i)][:].rearrange("w (a u) n -> w a n u", a=PASSES),
+                    in_=flipped_of[(b, s0 + i)][:].rearrange("w (a u) n -> w a n u", a=PASSES),
                 )
 
-        def quantise_xk(b, pair):
-            xk_grouped, xk_codes, xk_scales = xk_of[(b, pair)]
+        def quantise_xk(b, s0, n):
+            xk_grouped, xk_codes, xk_scales = xk_of[(b, s0)]
             nc.vector.quantize_mx(
-                out=xk_codes[:].rearrange("f s c n -> f (s c n)").bitcast(FP8X4),
-                scales=xk_scales[:].rearrange("f s c n -> f (s c n)"),
-                in_=xk_grouped[:],
+                out=xk_codes[:, 0:n].rearrange("f s c n -> f (s c n)").bitcast(FP8X4),
+                scales=xk_scales[:, 0:n].rearrange("f s c n -> f (s c n)"),
+                in_=xk_grouped[:, 0 : n * slot_cols],
             )
 
-        def multiply(b, pair):
-            xk_codes, xk_scales = xk_of[(b, pair)][1], xk_of[(b, pair)][2]
+        def multiply(b, s0, n):
+            xk_codes, xk_scales = xk_of[(b, s0)][1], xk_of[(b, s0)][2]
             summed = ps_gate.tile([P, 2, GATES * UNITS], F32)
-            for i in range(2):
+            for i in range(n):
                 for c in range(PASSES):
                     nc.tensor.matmul_mx(
                         out=summed[:, i, :],
@@ -291,67 +291,78 @@ def tile_gts_gcgrucell_pb_t_kernel(
                         start=(c == 0),
                         stop=(c == PASSES - 1),
                     )
-            summed_of[(b, pair)] = summed
+            summed_of[(b, s0)] = summed
 
-        def finish(b, pair):
-            if pair % 2 == 0:
+        def finish(b, s0, n):
+            g, t0 = divmod(s0, PACK)
+            if t0 == 0:
                 result = outs.tile([P, GATES, PACK, UNITS], F32)
                 result_of[b] = result
             result = result_of[b]
-            s0 = 2 * pair
-            i0 = s0 % PACK
             biased = outs.tile([P, 2, GATES * UNITS], F32)
             nc.vector.tensor_tensor(
-                out=biased[:],
-                in0=summed_of[(b, pair)][:],
-                in1=bias_bc[:].unsqueeze(1).to_broadcast([P, 2, GATES * UNITS]),
+                out=biased[:, 0:n, :],
+                in0=summed_of[(b, s0)][:, 0:n, :],
+                in1=bias_bc[:].unsqueeze(1).to_broadcast([P, n, GATES * UNITS]),
                 op=ALU.add,
             )
             nc.scalar.activation(
-                out=result[:, :, i0 : i0 + 2, :].rearrange("p g s j -> p s g j"),
-                in_=biased[:].rearrange("p s (g j) -> p s g j", g=GATES),
+                out=result[:, :, t0 : t0 + n, :].rearrange("p g s j -> p s g j"),
+                in_=biased[:, 0:n, :].rearrange("p s (g j) -> p s g j", g=GATES),
                 func=ACT.Sigmoid,
             )
             nc.gpsimd.tensor_tensor(
-                out=result[:, 0, i0 : i0 + 2, :],
-                in0=result[:, 0, i0 : i0 + 2, :],
-                in1=state_of[b][:, s0 : s0 + 2, :],
+                out=result[:, 0, t0 : t0 + n, :],
+                in0=result[:, 0, t0 : t0 + n, :],
+                in1=state_of[b][:, s0 : s0 + n, :],
                 op=ALU.mult,
             )
-            if pair % 2 == 1:
-                g = pair // 2
+            if b == BATCH - 1 and g == PASSES - 1:
+                first, count = t0, n
+            elif t0 + n == PACK:
+                first, count = 0, PACK
+            else:
+                first, count = 0, 0
+            if count:
                 for gate in range(GATES):
                     nc.sync.dma_start(
-                        out=by_node(out_rows[gate][b])[:, g, :],
-                        in_=result[:, gate].rearrange("p t j -> p (t j)"),
+                        out=by_node(out_rows[gate][b])[:, g, first * UNITS : (first + count) * UNITS],
+                        in_=result[:, gate, first : first + count, :].rearrange("p t j -> p (t j)"),
                     )
 
-        pairs = SLOTS // 2
-        ticks = BATCH * pairs
+        pieces = []
+        for b in range(BATCH):
+            for s0 in range(0, SLOTS, 2):
+                if (b, s0) in ((0, 0), (BATCH - 1, SLOTS - 2)):
+                    pieces.extend([(b, s0, 1), (b, s0 + 1, 1)])
+                else:
+                    pieces.append((b, s0, 2))
+        ticks = len(pieces)
         for tick in range(ticks + 4):
-            ahead = tick // pairs + 1
-            if tick % pairs == 0 and ahead + 1 < BATCH:
-                load_batch(ahead + 1)
-            if 3 <= tick < ticks + 3:
-                quantise_xk(*divmod(tick - 3, pairs))
             if tick < ticks:
-                diffuse(*divmod(tick, pairs))
-            if tick < 2:
-                quantise_adj(tick + 2)
-            if 1 <= tick < ticks + 1:
-                flip(*divmod(tick - 1, pairs))
-            if 2 <= tick < ticks + 2:
-                gather(*divmod(tick - 2, pairs))
+                b, s0, n = pieces[tick]
+                if s0 == 0 and b + 2 < BATCH:
+                    load_batch(b + 2)
             if 3 <= tick < ticks + 3:
-                multiply(*divmod(tick - 3, pairs))
+                quantise_xk(*pieces[tick - 3])
+            if tick < ticks:
+                diffuse(*pieces[tick])
+            if tick < 2:
+                quantise_adj(2 * tick + 4, 2)
+            if 1 <= tick < ticks + 1:
+                flip(*pieces[tick - 1])
+            if 2 <= tick < ticks + 2:
+                gather(*pieces[tick - 2])
+            if 3 <= tick < ticks + 3:
+                multiply(*pieces[tick - 3])
             if 4 <= tick:
-                finish(*divmod(tick - 4, pairs))
-            if ahead < BATCH:
-                if tick % pairs == 0:
-                    place_features(ahead, 2)
-                if tick % pairs == 1:
-                    group_x2(ahead)
-                    place_features(ahead, 1)
-                if tick % pairs == 2:
-                    quantise_x2(ahead)
-                    place_features(ahead, 0)
+                finish(*pieces[tick - 4])
+            if tick < ticks and b + 1 < BATCH:
+                if s0 == 0:
+                    place_features(b + 1, 2)
+                if s0 == 2:
+                    group_x2(b + 1)
+                    place_features(b + 1, 1)
+                if s0 == 4:
+                    quantise_x2(b + 1)
+                    place_features(b + 1, 0)

@@ -64,12 +64,15 @@ def tile_gts_gcgrucell_pb_t_kernel(
         summed_of = {}
         result_of = {}
 
-        def load_term(b, k):
-            x_raw = loads.tile([P, SLOTS, FEATS], BF16, name="x%d_raw" % k)
+        def load_term(b, k, halves=(0, 1)):
+            if k not in loaded_of[b]:
+                x_raw = loads.tile([P, SLOTS, FEATS], BF16, name="x%d_raw" % k)
+                loaded_of[b][k] = x_raw
+            g0, g1 = halves[0], halves[-1] + 1
             nc.sync.dma_start(
-                out=x_raw[:].rearrange("p (g t) f -> p g (t f)", g=PASSES), in_=by_node(x_dram[k][b])
+                out=loaded_of[b][k][:, g0 * PACK : g1 * PACK, :].rearrange("p (g t) f -> p g (t f)", t=PACK),
+                in_=by_node(x_dram[k][b])[:, g0:g1, :],
             )
-            loaded_of[b][k] = x_raw
 
         def load_state(b):
             h_sb = states.tile([P, SLOTS, UNITS], BF16)
@@ -85,20 +88,22 @@ def tile_gts_gcgrucell_pb_t_kernel(
                 load_term(b, k)
             load_state(b)
 
-        def place_features(b, k):
-            x_raw = loaded_of[b][k]
-            x_sb = terms.tile([P, SLOTS, FEATS], BF16, name="x%d_sb" % k)
+        def place_features(b, k, halves=(0, 1)):
+            if k not in terms_of[b]:
+                x_sb = terms.tile([P, SLOTS, FEATS], BF16, name="x%d_sb" % k)
+                terms_of[b][k] = x_sb
+            slots = slice(halves[0] * PACK, (halves[-1] + 1) * PACK)
             nc.vector.tensor_copy(
-                out=x_sb[:].rearrange("p s (c j i) -> p c s j i", c=CLASSES, i=RUN),
-                in_=x_raw[:].rearrange("p s (j c i) -> p c s j i", c=CLASSES, i=RUN),
+                out=terms_of[b][k][:, slots, :].rearrange("p s (c j i) -> p c s j i", c=CLASSES, i=RUN),
+                in_=loaded_of[b][k][:, slots, :].rearrange("p s (j c i) -> p c s j i", c=CLASSES, i=RUN),
             )
-            terms_of[b][k] = x_sb
 
         def group_x2(b):
             x2_sb = terms_of[b][2]
             x2_grouped = work.tile([P, PASSES, FEATS, PACK], BF16, align_bytes=64)
             for g in range(PASSES):
-                nc.scalar.copy(
+                copy = nc.vector.tensor_copy if (b, g) == (0, 1) else nc.scalar.copy
+                copy(
                     out=x2_grouped[:, g].rearrange("p (c i) t -> p c t i", i=4),
                     in_=x2_sb[:, g * PACK : (g + 1) * PACK, :].rearrange("p t (c i) -> p c t i", i=4),
                 )
@@ -123,16 +128,19 @@ def tile_gts_gcgrucell_pb_t_kernel(
             cols = slice(t * NODES, (t + n) * NODES)
             nc.sync.dma_start(out=adj_sb[:, g, cols], in_=by_node(adj)[:, g, cols])
 
-        load_term(0, 2)
+        load_term(0, 2, (0,))
+        load_term(0, 2, (1,))
         load_adj(0, 1)
         load_adj(1, 1)
-        load_adj(2, 2)
-        load_term(0, 1)
+        load_term(0, 1, (0,))
+        load_term(0, 0, (0,))
         rows_here = TERMS * FEATS // P
         w_raw = const.tile([P, GATES, rows_here * UNITS], BF16)
         for gate, kernel in enumerate((r_kernel, u_kernel)):
             nc.sync.dma_start(out=w_raw[:, gate, :], in_=kernel.rearrange("(p r) j -> p (r j)", p=P))
-        load_term(0, 0)
+        load_adj(2, 2)
+        load_term(0, 1, (1,))
+        load_term(0, 0, (1,))
         load_adj(4, 2)
         load_adj(6, 2)
         bias_row = const.tile([P, GATES * UNITS], BF16)
@@ -147,7 +155,8 @@ def tile_gts_gcgrucell_pb_t_kernel(
         ident_bf = const.tile([P, P], BF16)
         make_identity(nc, ident_bf[:])
 
-        place_features(0, 2)
+        place_features(0, 2, (0,))
+        place_features(0, 2, (1,))
         group_x2(0)
         quantise_x2(0)
 
@@ -178,9 +187,11 @@ def tile_gts_gcgrucell_pb_t_kernel(
 
         quantise_adj(0, 1)
         quantise_adj(1, 1)
+        place_features(0, 1, (0,))
+        place_features(0, 0, (0,))
         quantise_adj(2, 2)
-        place_features(0, 1)
-        place_features(0, 0)
+        place_features(0, 1, (1,))
+        place_features(0, 0, (1,))
 
         shuffle = const.tile([P, P], BF16)
         nc.vector.tensor_copy(

@@ -177,8 +177,7 @@ def tile_gts_gcgrucell_pb_t_kernel(
                 for c in range(PASSES):
                     for u in range(2):
                         nc.tensor.transpose(adj_flipped[:, c, u, :], adj_words[:, s, c, u, :], ident_f32[:])
-                copy = nc.vector.tensor_copy if s % 2 == 0 else nc.scalar.copy
-                copy(out=adj_grouped_words[:, s], in_=adj_flipped[:].rearrange("q c u n -> q c n u"))
+                nc.scalar.copy(out=adj_grouped_words[:, s], in_=adj_flipped[:].rearrange("q c u n -> q c n u"))
             nc.vector.quantize_mx(
                 out=adj_codes[:, s0 : s0 + n].rearrange("q s c n -> q (s c n)").bitcast(FP8X4),
                 scales=adj_scales[:, s0 : s0 + n].rearrange("q s c n -> q (s c n)"),

@@ -93,9 +93,15 @@ def tile_gts_gcgrucell_pb_t_kernel(
                 x_sb = terms.tile([P, SLOTS, FEATS], BF16, name="x%d_sb" % k)
                 terms_of[b][k] = x_sb
             slots = slice(halves[0] * PACK, (halves[-1] + 1) * PACK)
-            nc.vector.tensor_copy(
-                out=terms_of[b][k][:, slots, :].rearrange("p s (c j i) -> p c s j i", c=CLASSES, i=RUN),
-                in_=loaded_of[b][k][:, slots, :].rearrange("p s (j c i) -> p c s j i", c=CLASSES, i=RUN),
+            placed = terms_of[b][k][:, slots, :].rearrange("p s f -> p (s f)")
+            raw = loaded_of[b][k][:, slots, :].rearrange("p s f -> p (s f)")
+            if k == 0 and b in (2, 5):
+                copy, placed, raw, run = nc.scalar.copy, placed.bitcast(F32), raw.bitcast(F32), RUN // 2
+            else:
+                copy, run = nc.vector.tensor_copy, RUN
+            copy(
+                out=placed.rearrange("p (s c j i) -> p c s j i", c=CLASSES, j=STRETCHES, i=run),
+                in_=raw.rearrange("p (s j c i) -> p c s j i", c=CLASSES, j=STRETCHES, i=run),
             )
 
         def group_x2(b):
@@ -118,6 +124,10 @@ def tile_gts_gcgrucell_pb_t_kernel(
                 in_=x2_grouped_of[b][:].rearrange("p g f t -> p (g f t)"),
             )
             x2_mx_of[b] = (x2_codes, x2_scales)
+
+        first_sigmoid = const.tile([P, 1], F32)
+        nc.gpsimd.memset(first_sigmoid[:], 0.0)
+        nc.scalar.activation(out=first_sigmoid[:], in_=first_sigmoid[:], func=ACT.Sigmoid)
 
         loaded_of[0] = {}
         terms_of[0] = {}
@@ -202,21 +212,21 @@ def tile_gts_gcgrucell_pb_t_kernel(
         w_scales = const.tile([P, PASSES, GATES * UNITS], U8, align_bytes=64)
 
         def quantise_kernels():
-            half = rows_here * UNITS // 2
             for gate in range(GATES):
-                w_moved = ps_flip.tile([P, rows_here * UNITS], BF16, tag="flip")
-                for i in range(2):
+                w_moved = ps_flip.tile([P, PASSES, UNITS, PACK], BF16, tag="flip")
+                rows = w_raw[:, gate, :].rearrange("p (e a u j) -> p a j u e", e=2, a=PASSES, u=2)
+                for a in range(PASSES):
                     nc.tensor.matmul(
-                        out=w_moved[:, i * half : (i + 1) * half],
+                        out=w_moved[:, a].rearrange("w j t -> w (j t)"),
                         lhsT=shuffle[:],
-                        rhs=w_raw[:, gate, i * half : (i + 1) * half],
+                        rhs=rows[:, a],
                         start=True,
                         stop=True,
                     )
                 for a in range(PASSES):
                     nc.scalar.copy(
-                        out=w_grouped[:, a, gate].rearrange("w j (u e) -> w j u e", e=2),
-                        in_=w_moved[:].rearrange("w (e a u j) -> w a j u e", e=2, a=PASSES, u=2)[:, a],
+                        out=w_grouped[:, a, gate].rearrange("w j t -> w (j t)").bitcast(F32),
+                        in_=w_moved[:, a].rearrange("w j t -> w (j t)").bitcast(F32),
                     )
             nc.vector.quantize_mx(
                 out=w_codes[:].rearrange("p c j -> p (c j)").bitcast(FP8X4),

@@ -95,7 +95,7 @@ def tile_gts_gcgrucell_pb_t_kernel(
             slots = slice(halves[0] * PACK, (halves[-1] + 1) * PACK)
             placed = terms_of[b][k][:, slots, :].rearrange("p s f -> p (s f)")
             raw = loaded_of[b][k][:, slots, :].rearrange("p s f -> p (s f)")
-            if k == 0 and b in (2, 5):
+            if (b, k) == (4, 0):
                 copy, placed, raw, run = nc.scalar.copy, placed.bitcast(F32), raw.bitcast(F32), RUN // 2
             else:
                 copy, run = nc.vector.tensor_copy, RUN
@@ -212,21 +212,21 @@ def tile_gts_gcgrucell_pb_t_kernel(
         w_scales = const.tile([P, PASSES, GATES * UNITS], U8, align_bytes=64)
 
         def quantise_kernels():
+            half = rows_here * UNITS // 2
             for gate in range(GATES):
-                w_moved = ps_flip.tile([P, PASSES, UNITS, PACK], BF16, tag="flip")
-                rows = w_raw[:, gate, :].rearrange("p (e a u j) -> p a j u e", e=2, a=PASSES, u=2)
-                for a in range(PASSES):
+                w_moved = ps_flip.tile([P, rows_here * UNITS], BF16, tag="flip")
+                for i in range(2):
                     nc.tensor.matmul(
-                        out=w_moved[:, a].rearrange("w j t -> w (j t)"),
+                        out=w_moved[:, i * half : (i + 1) * half],
                         lhsT=shuffle[:],
-                        rhs=rows[:, a],
+                        rhs=w_raw[:, gate, i * half : (i + 1) * half],
                         start=True,
                         stop=True,
                     )
                 for a in range(PASSES):
                     nc.scalar.copy(
-                        out=w_grouped[:, a, gate].rearrange("w j t -> w (j t)").bitcast(F32),
-                        in_=w_moved[:, a].rearrange("w j t -> w (j t)").bitcast(F32),
+                        out=w_grouped[:, a, gate].rearrange("w j (u e) -> w j u e", e=2),
+                        in_=w_moved[:].rearrange("w (e a u j) -> w a j u e", e=2, a=PASSES, u=2)[:, a],
                     )
             nc.vector.quantize_mx(
                 out=w_codes[:].rearrange("p c j -> p (c j)").bitcast(FP8X4),

@@ -157,8 +157,13 @@ def tile_gts_gcgrucell_pb_t_kernel(
         nc.gpsimd.memset(bias_row[:], 0.0)
         nc.sync.dma_start(out=bias_row[0:1, 0:UNITS], in_=r_bias.rearrange("(o j) -> o j", o=1))
         nc.sync.dma_start(out=bias_row[0:1, UNITS : 2 * UNITS], in_=u_bias.rearrange("(o j) -> o j", o=1))
+        loaded_of[1] = {}
+        terms_of[1] = {}
+        load_term(1, 2)
         load_state(0)
-        load_batch(1)
+        load_term(1, 1)
+        load_term(1, 0)
+        load_state(1)
 
         ident_f32 = const.tile([P, P], F32)
         make_identity(nc, ident_f32[:])
@@ -331,7 +336,8 @@ def tile_gts_gcgrucell_pb_t_kernel(
                 in_=biased[:, 0:n, :].rearrange("p s (g j) -> p s g j", g=GATES),
                 func=ACT.Sigmoid,
             )
-            nc.gpsimd.tensor_tensor(
+            engine = nc.vector if b == BATCH - 1 and s0 >= SLOTS - 2 else nc.gpsimd
+            engine.tensor_tensor(
                 out=result[:, 0, t0 : t0 + n, :],
                 in0=result[:, 0, t0 : t0 + n, :],
                 in1=state_of[b][:, s0 : s0 + n, :],
@@ -344,7 +350,7 @@ def tile_gts_gcgrucell_pb_t_kernel(
             else:
                 first, count = 0, 0
             if count:
-                for gate in range(GATES):
+                for gate in (1, 0):
                     nc.sync.dma_start(
                         out=by_node(out_rows[gate][b])[:, g, first * UNITS : (first + count) * UNITS],
                         in_=result[:, gate, first : first + count, :].rearrange("p t j -> p (t j)"),

from contextlib import ExitStack

import concourse.mybir as mybir
from concourse.masks import make_identity

BF16 = mybir.dt.bfloat16
F32 = mybir.dt.float32
U32 = mybir.dt.uint32
U8 = mybir.dt.uint8
FP8X4 = mybir.dt.float8_e4m3fn_x4
ALU = mybir.AluOpType
ACT = mybir.ActivationFunctionType

P = 128
PACK = 4
BATCH = 8
NODES = 1024
FEATS = 256
UNITS = 128
TERMS = 4
PASSES = 2
SLOTS = NODES // P
GATES = 2
RUN = 8
CLASSES = 4
STRETCHES = FEATS // (RUN * CLASSES)
LEAD = 3

FLOPS = 2 * BATCH * NODES * NODES * FEATS + 2 * BATCH * NODES * (TERMS * FEATS) * (GATES * UNITS)


def by_node(rows):
    return rows.rearrange("(g p t) w -> p g (t w)", g=PASSES, p=P, t=PACK)


def tile_gts_gcgrucell_pb_t_kernel(
    tc, adj, x0, x1, x2, h_prev, r_kernel, r_bias, u_kernel, u_bias, out_0, out_1
):
    nc = tc.nc
    with ExitStack() as ctx:
        const = ctx.enter_context(tc.tile_pool(name="const", bufs=1))
        loads = ctx.enter_context(tc.tile_pool(name="loads", bufs=2))
        states = ctx.enter_context(tc.tile_pool(name="states", bufs=LEAD + 3))
        terms = ctx.enter_context(tc.tile_pool(name="terms", bufs=LEAD + 2))
        spread_out = ctx.enter_context(tc.tile_pool(name="spread_out", bufs=3))
        work = ctx.enter_context(tc.tile_pool(name="work", bufs=2))
        pairs_pool = ctx.enter_context(tc.tile_pool(name="pairs_pool", bufs=3))
        outs = ctx.enter_context(tc.tile_pool(name="outs", bufs=3))
        ps_flip = ctx.enter_context(tc.psum_pool(name="ps_flip", bufs=4))
        ps_diff = ctx.enter_context(tc.psum_pool(name="ps_diff", bufs=2))
        ps_gate = ctx.enter_context(tc.psum_pool(name="ps_gate", bufs=2))

        x_dram = [x0, x1, x2]
        h_rows = h_prev.rearrange("b (n j) -> b n j", j=UNITS)
        out_rows = [out_0, out_1.rearrange("b (n j) -> b n j", j=UNITS)]

        loaded_of = {}
        terms_of = {}
        state_of = {}
        x2_grouped_of = {}
        x2_mx_of = {}
        flipped_of = {}
        xk_of = {}
        summed_of = {}
        result_of = {}

        def load_term(b, k, halves=(0, 1)):
            if k not in loaded_of[b]:
                x_raw = loads.tile([P, SLOTS, FEATS], BF16, name="x%d_raw" % k)
                loaded_of[b][k] = x_raw
            g0, g1 = halves[0], halves[-1] + 1
            nc.sync.dma_start(
                out=loaded_of[b][k][:, g0 * PACK : g1 * PACK, :].rearrange("p (g t) f -> p g (t f)", t=PACK),
                in_=by_node(x_dram[k][b])[:, g0:g1, :],
            )

        def load_state(b):
            h_sb = states.tile([P, SLOTS, UNITS], BF16)
            nc.sync.dma_start(
                out=h_sb[:].rearrange("p (g t) j -> p g (t j)", g=PASSES), in_=by_node(h_rows[b])
            )
            state_of[b] = h_sb

        def load_batch(b):
            loaded_of[b] = {}
            terms_of[b] = {}
            for k in (2, 1, 0):
                load_term(b, k)
            load_state(b)

        def place_features(b, k, halves=(0, 1)):
            if k not in terms_of[b]:
                x_sb = terms.tile([P, SLOTS, FEATS], BF16, name="x%d_sb" % k)
                terms_of[b][k] = x_sb
            slots = slice(halves[0] * PACK, (halves[-1] + 1) * PACK)
            placed = terms_of[b][k][:, slots, :].rearrange("p s f -> p (s f)")
            raw = loaded_of[b][k][:, slots, :].rearrange("p s f -> p (s f)")
            if (b, k) == (4, 0):
                copy, placed, raw, run = nc.scalar.copy, placed.bitcast(F32), raw.bitcast(F32), RUN // 2
            else:
                copy, run = nc.vector.tensor_copy, RUN
            copy(
                out=placed.rearrange("p (s c j i) -> p c s j i", c=CLASSES, j=STRETCHES, i=run),
                in_=raw.rearrange("p (s j c i) -> p c s j i", c=CLASSES, j=STRETCHES, i=run),
            )

        def group_x2(b):
            x2_sb = terms_of[b][2]
            x2_grouped = work.tile([P, PASSES, FEATS, PACK], BF16, align_bytes=64)
            for g in range(PASSES):
                copy = nc.vector.tensor_copy if (b, g) == (0, 1) else nc.scalar.copy
                copy(
                    out=x2_grouped[:, g].rearrange("p (c i) t -> p c t i", i=4),
                    in_=x2_sb[:, g * PACK : (g + 1) * PACK, :].rearrange("p t (c i) -> p c t i", i=4),
                )
            x2_grouped_of[b] = x2_grouped

        def quantise_x2(b):
            x2_codes = terms.tile([P, PASSES, FEATS], U32, align_bytes=64)
            x2_scales = terms.tile([P, PASSES, FEATS], U8, align_bytes=64)
            nc.vector.quantize_mx(
                out=x2_codes[:].rearrange("p g f -> p (g f)").bitcast(FP8X4),
                scales=x2_scales[:].rearrange("p g f -> p (g f)"),
                in_=x2_grouped_of[b][:].rearrange("p g f t -> p (g f t)"),
            )
            x2_mx_of[b] = (x2_codes, x2_scales)

        first_sigmoid = const.tile([P, 1], F32)
        nc.gpsimd.memset(first_sigmoid[:], 0.0)
        nc.scalar.activation(out=first_sigmoid[:], in_=first_sigmoid[:], func=ACT.Sigmoid)

        loaded_of[0] = {}
        terms_of[0] = {}
        adj_sb = const.tile([P, PASSES, PACK * NODES], BF16)

        def load_adj(s0, n):
            g, t = divmod(s0, PACK)
            cols = slice(t * NODES, (t + n) * NODES)
            nc.sync.dma_start(out=adj_sb[:, g, cols], in_=by_node(adj)[:, g, cols])

        load_term(0, 2, (0,))
        load_term(0, 2, (1,))
        load_adj(0, 1)
        load_adj(1, 1)
        load_term(0, 1, (0,))
        load_term(0, 0, (0,))
        rows_here = TERMS * FEATS // P
        w_raw = const.tile([P, GATES, rows_here * UNITS], BF16)
        for gate, kernel in enumerate((r_kernel, u_kernel)):
            nc.sync.dma_start(out=w_raw[:, gate, :], in_=kernel.rearrange("(p r) j -> p (r j)", p=P))
        load_adj(2, 2)
        load_term(0, 1, (1,))
        load_term(0, 0, (1,))
        load_adj(4, 2)
        load_adj(6, 2)
        bias_row = const.tile([P, GATES * UNITS], BF16)
        nc.gpsimd.memset(bias_row[:], 0.0)
        nc.sync.dma_start(out=bias_row[0:1, 0:UNITS], in_=r_bias.rearrange("(o j) -> o j", o=1))
        nc.sync.dma_start(out=bias_row[0:1, UNITS : 2 * UNITS], in_=u_bias.rearrange("(o j) -> o j", o=1))
        loaded_of[1] = {}
        terms_of[1] = {}
        load_term(1, 2)
        load_state(0)
        load_term(1, 1)
        load_term(1, 0)
        load_state(1)

        ident_f32 = const.tile([P, P], F32)
        make_identity(nc, ident_f32[:])
        ident_bf = const.tile([P, P], BF16)
        make_identity(nc, ident_bf[:])

        place_features(0, 2, (0,))
        place_features(0, 2, (1,))
        group_x2(0)
        quantise_x2(0)

        adj_words = adj_sb[:].rearrange("p g w -> p (g w)").bitcast(F32).rearrange(
            "p (s c q u) -> p s c u q", s=SLOTS, c=PASSES, q=P, u=2
        )
        adj_grouped = const.tile([P, SLOTS * PASSES * P * PACK], BF16, align_bytes=64)
        adj_grouped_words = adj_grouped[:].bitcast(F32).rearrange(
            "q (s c n u) -> q s c n u", s=SLOTS, c=PASSES, n=P, u=2
        )
        adj_codes = const.tile([P, SLOTS, PASSES, P], U32, align_bytes=64)
        adj_scales = const.tile([P, SLOTS, PASSES, P], U8, align_bytes=64)
        slot_cols = PASSES * P * PACK

        def quantise_adj(s0, n):
            for s in range(s0, s0 + n):
                adj_flipped = ps_flip.tile([P, PASSES, 2, P], F32, tag="flip")
                for c in range(PASSES):
                    for u in range(2):
                        nc.tensor.transpose(adj_flipped[:, c, u, :], adj_words[:, s, c, u, :], ident_f32[:])
                nc.scalar.copy(out=adj_grouped_words[:, s], in_=adj_flipped[:].rearrange("q c u n -> q c n u"))
            nc.vector.quantize_mx(
                out=adj_codes[:, s0 : s0 + n].rearrange("q s c n -> q (s c n)").bitcast(FP8X4),
                scales=adj_scales[:, s0 : s0 + n].rearrange("q s c n -> q (s c n)"),
                in_=adj_grouped[:, s0 * slot_cols : (s0 + n) * slot_cols],
            )

        quantise_adj(0, 1)
        quantise_adj(1, 1)
        place_features(0, 1, (0,))
        place_features(0, 0, (0,))
        quantise_adj(2, 2)
        place_features(0, 1, (1,))
        place_features(0, 0, (1,))

        shuffle = const.tile([P, P], BF16)
        nc.vector.tensor_copy(
            out=shuffle[:].rearrange("k (c j i) -> k c j i", c=CLASSES, j=STRETCHES),
            in_=ident_bf[:].rearrange("k (j c i) -> k c j i", c=CLASSES, j=STRETCHES),
        )
        w_grouped = const.tile([P, PASSES, GATES, UNITS, PACK], BF16, align_bytes=64)
        w_codes = const.tile([P, PASSES, GATES * UNITS], U32, align_bytes=64)
        w_scales = const.tile([P, PASSES, GATES * UNITS], U8, align_bytes=64)

        def quantise_kernels():
            half = rows_here * UNITS // 2
            for gate in range(GATES):
                w_moved = ps_flip.tile([P, rows_here * UNITS], BF16, tag="flip")
                for i in range(2):
                    nc.tensor.matmul(
                        out=w_moved[:, i * half : (i + 1) * half],
                        lhsT=shuffle[:],
                        rhs=w_raw[:, gate, i * half : (i + 1) * half],
                        start=True,
                        stop=True,
                    )
                for a in range(PASSES):
                    nc.scalar.copy(
                        out=w_grouped[:, a, gate].rearrange("w j (u e) -> w j u e", e=2),
                        in_=w_moved[:].rearrange("w (e a u j) -> w a j u e", e=2, a=PASSES, u=2)[:, a],
                    )
            nc.vector.quantize_mx(
                out=w_codes[:].rearrange("p c j -> p (c j)").bitcast(FP8X4),
                scales=w_scales[:].rearrange("p c j -> p (c j)"),
                in_=w_grouped[:].rearrange("p c g j t -> p (c g j t)"),
            )

        quantise_kernels()

        ones = const.tile([P, P], BF16)
        nc.gpsimd.memset(ones[:], 1.0)
        bias_sum = ps_gate.tile([P, 2, GATES * UNITS], F32, tag="summed")
        nc.tensor.matmul(out=bias_sum[:, 0, :], lhsT=ones[:], rhs=bias_row[:], start=True, stop=True)
        bias_bc = const.tile([P, GATES * UNITS], F32)
        nc.scalar.copy(out=bias_bc[:], in_=bias_sum[:, 0, :])


        def diffuse(b, s0, n):
            if s0 == 0:
                x3_sb = spread_out.tile([P, SLOTS, FEATS], BF16)
                terms_of[b][3] = x3_sb
            x2_codes, x2_scales = x2_mx_of[b]
            spread = ps_diff.tile([P, 2, FEATS], F32)
            for i in range(n):
                for c in range(PASSES):
                    nc.tensor.matmul_mx(
                        out=spread[:, i, :],
                        lhsT=adj_codes[:, s0 + i, c, :].bitcast(FP8X4),
                        lhsT_scale=adj_scales[:, s0 + i, c, :],
                        rhs=x2_codes[:, c, :].bitcast(FP8X4),
                        rhs_scale=x2_scales[:, c, :],
                        start=(c == 0),
                        stop=(c == PASSES - 1),
                    )
            nc.vector.scalar_tensor_tensor(
                out=terms_of[b][3][:, s0 : s0 + n, :],
                in0=spread[:, 0:n, :],
                scalar=2.0,
                in1=terms_of[b][1][:, s0 : s0 + n, :],
                op0=ALU.mult,
                op1=ALU.subtract,
            )

        def flip(b, s0, n):
            for s in range(s0, s0 + n):
                flipped = ps_flip.tile([P, TERMS, P], F32, tag="flip")
                for k in range(TERMS):
                    nc.tensor.transpose(flipped[:, k, :], terms_of[b][k][:, s, :].bitcast(F32), ident_f32[:])
                flipped_of[(b, s)] = flipped

        def gather(b, s0, n):
            xk_grouped = pairs_pool.tile([P, 2 * slot_cols], BF16, align_bytes=64)
            xk_codes = pairs_pool.tile([P, 2, PASSES, P], U32, align_bytes=64)
            xk_scales = pairs_pool.tile([P, 2, PASSES, P], U8, align_bytes=64)
            xk_of[(b, s0)] = (xk_grouped, xk_codes, xk_scales)
            xk_words = xk_grouped[:].bitcast(F32).rearrange("w (s a n u) -> w s a n u", s=2, a=PASSES, n=P, u=2)
            for i in range(n):
                nc.scalar.copy(
                    out=xk_words[:, i],
                    in_=flipped_of[(b, s0 + i)][:].rearrange("w (a u) n -> w a n u", a=PASSES),
                )

        def quantise_xk(b, s0, n):
            xk_grouped, xk_codes, xk_scales = xk_of[(b, s0)]
            nc.vector.quantize_mx(
                out=xk_codes[:, 0:n].rearrange("f s c n -> f (s c n)").bitcast(FP8X4),
                scales=xk_scales[:, 0:n].rearrange("f s c n -> f (s c n)"),
                in_=xk_grouped[:, 0 : n * slot_cols],
            )

        def multiply(b, s0, n):
            xk_codes, xk_scales = xk_of[(b, s0)][1], xk_of[(b, s0)][2]
            summed = ps_gate.tile([P, 2, GATES * UNITS], F32)
            for i in range(n):
                for c in range(PASSES):
                    nc.tensor.matmul_mx(
                        out=summed[:, i, :],
                        lhsT=xk_codes[:, i, c, :].bitcast(FP8X4),
                        lhsT_scale=xk_scales[:, i, c, :],
                        rhs=w_codes[:, c, :].bitcast(FP8X4),
                        rhs_scale=w_scales[:, c, :],
                        start=(c == 0),
                        stop=(c == PASSES - 1),
                    )
            summed_of[(b, s0)] = summed

        def finish(b, s0, n):
            g, t0 = divmod(s0, PACK)
            if t0 == 0:
                result = outs.tile([P, GATES, PACK, UNITS], F32)
                result_of[b] = result
            result = result_of[b]
            biased = outs.tile([P, 2, GATES * UNITS], F32)
            nc.vector.tensor_tensor(
                out=biased[:, 0:n, :],
                in0=summed_of[(b, s0)][:, 0:n, :],
                in1=bias_bc[:].unsqueeze(1).to_broadcast([P, n, GATES * UNITS]),
                op=ALU.add,
            )
            nc.scalar.activation(
                out=result[:, :, t0 : t0 + n, :].rearrange("p g s j -> p s g j"),
                in_=biased[:, 0:n, :].rearrange("p s (g j) -> p s g j", g=GATES),
                func=ACT.Sigmoid,
            )
            engine = nc.vector if b == BATCH - 1 and s0 >= SLOTS - 2 else nc.gpsimd
            engine.tensor_tensor(
                out=result[:, 0, t0 : t0 + n, :],
                in0=result[:, 0, t0 : t0 + n, :],
                in1=state_of[b][:, s0 : s0 + n, :],
                op=ALU.mult,
            )
            if b == BATCH - 1 and g == PASSES - 1:
                first, count = t0, n
            elif t0 + n == PACK:
                first, count = 0, PACK
            else:
                first, count = 0, 0
            if count:
                for gate in (1, 0):
                    nc.sync.dma_start(
                        out=by_node(out_rows[gate][b])[:, g, first * UNITS : (first + count) * UNITS],
                        in_=result[:, gate, first : first + count, :].rearrange("p t j -> p (t j)"),
                    )

        pieces = []
        for b in range(BATCH):
            for s0 in range(0, SLOTS, 2):
                if (b, s0) in ((0, 0), (BATCH - 1, SLOTS - 2)):
                    pieces.extend([(b, s0, 1), (b, s0 + 1, 1)])
                else:
                    pieces.append((b, s0, 2))
        ticks = len(pieces)
        for tick in range(ticks + 4):
            if tick < ticks:
                b, s0, n = pieces[tick]
                if s0 == 0 and b + 2 < BATCH:
                    load_batch(b + 2)
            if 3 <= tick < ticks + 3:
                quantise_xk(*pieces[tick - 3])
            if tick < ticks:
                diffuse(*pieces[tick])
            if tick < 2:
                quantise_adj(2 * tick + 4, 2)
            if 1 <= tick < ticks + 1:
                flip(*pieces[tick - 1])
            if 2 <= tick < ticks + 2:
                gather(*pieces[tick - 2])
            if 3 <= tick < ticks + 3:
                multiply(*pieces[tick - 3])
            if 4 <= tick:
                finish(*pieces[tick - 4])
            if tick < ticks and b + 1 < BATCH:
                if s0 == 0:
                    place_features(b + 1, 2)
                if s0 == 2:
                    group_x2(b + 1)
                    place_features(b + 1, 1)
                if s0 == 4:
                    quantise_x2(b + 1)
                    place_features(b + 1, 0)
